import numpy as np
import ml_dtypes


def mxq(x, axis, fmt="e4m3"):
    dtype, down = {"e4m3": (ml_dtypes.float8_e4m3fn, 7), "e5m2": (ml_dtypes.float8_e5m2, 14)}[fmt]
    v = np.moveaxis(np.asarray(x, np.float32).astype(ml_dtypes.bfloat16).astype(np.float64), axis, -1)
    blocks = v.reshape(v.shape[:-1] + (-1, 32))
    amax = np.abs(blocks).max(-1, keepdims=True)
    byte = np.maximum(np.where(amax > 0, np.frexp(amax)[1] - 1 + 127, 0) - down, 1)
    scale = np.exp2(byte - 127.0)
    codes = (blocks / scale).astype(np.float32).astype(dtype).astype(np.float64)
    return np.moveaxis((codes * scale).reshape(v.shape), -1, axis)


WIDE = False


def mx_kscale(k):
    if not WIDE:
        return np.ones(k)
    levels = np.array([10, -10, 5, -5, 0])
    a = np.random.permutation(np.resize(levels, k // 512 * 4)).reshape(k // 512, 4)
    idx = np.arange(k)
    return np.exp2(a[idx // 512, idx % 128 // 32])


BF16 = ml_dtypes.bfloat16


def bf(x):
    return np.asarray(x, np.float32).astype(BF16)


def f64(x):
    return np.asarray(x).astype(np.float64)


B, S, K, IN, HID, OUT = 4, 128, 16, 1024, 512, 127
LN_EPS = 1e-5
LINK_EPS = 1e-8


def sigmoid(v):
    return 1.0 / (1.0 + np.exp(-v))


def setup_inputs():
    s, t = mx_kscale(IN), mx_kscale(HID)
    keep = np.random.random((B, S, 1, 1)) > 0.125
    return {"net_in": bf(np.random.standard_normal((B, S, K, IN)) * s),
            "embeds": bf(np.random.standard_normal((B, S, OUT)) * 0.5),
            "m": bf(np.random.random((B, S, K, 1)) * keep),
            "W1": bf(np.random.standard_normal((IN, HID)) / np.sqrt(IN) / s[:, None] * t),
            "b1": bf(np.random.standard_normal(HID) * 0.3 * t),
            "Wf": bf(np.random.standard_normal((HID, OUT + 1)) * 3.0 / np.sqrt(HID) / t[:, None]),
            "b_f": bf(np.random.standard_normal(OUT + 1) * 0.3),
            "gamma": bf(1.0 + 0.1 * np.random.standard_normal(OUT)),
            "beta": bf(0.1 * np.random.standard_normal(OUT))}


def reference(net_in, embeds, m, W1, b1, Wf, b_f, gamma, beta):
    h = np.maximum((mxq(f64(net_in), 3, "e4m3") @ mxq(f64(W1), 0, "e4m3")) + f64(b1), 0.0)
    out = (mxq(h, 3, "e4m3") @ mxq(f64(Wf), 0, "e4m3")) + f64(b_f)
    out = np.concatenate([out[..., :-1], sigmoid(out[..., -1:])], axis=-1)
    out = f64(m) * out
    link_weight = out[..., -1] + LINK_EPS
    norm = link_weight.sum(axis=2, keepdims=True)
    weights = (link_weight / norm)[..., None]
    updates = (out * weights).sum(axis=2)
    upd_weights = updates[..., -1:]
    embeds_new = f64(embeds) + upd_weights * updates[..., :-1]
    mu = embeds_new.mean(axis=-1, keepdims=True)
    var = ((embeds_new - mu) ** 2).mean(axis=-1, keepdims=True)
    return (embeds_new - mu) / np.sqrt(var + LN_EPS) * f64(gamma) + f64(beta)

@@ -1,0 +1,299 @@
+from contextlib import ExitStack
+
+import concourse.mybir as mybir
+from concourse.masks import make_identity
+
+F32 = mybir.dt.float32
+BF16 = mybir.dt.bfloat16
+U32 = mybir.dt.uint32
+U8 = mybir.dt.uint8
+FP8X4 = mybir.dt.float8_e4m3fn_x4
+ALU = mybir.AluOpType
+ACT = mybir.ActivationFunctionType
+AX = mybir.AxisListType
+
+P = 128
+B, S, K, IN, HID, OUT = 4, 128, 16, 1024, 512, 127
+CH = OUT + 1
+LPC = 4
+NCH = B * K // LPC
+ROWS = LPC * P
+LN_EPS = 1e-5
+LINK_EPS = 1e-8
+
+FLOPS = 2 * B * S * K * IN * HID + 2 * B * S * K * HID * CH
+
+LOOK = 2
+
+
+def tile_embed_update_pa_t_kernel(tc, net_in, embeds, m, W1, b1, Wf, b_f, gamma, beta, out):
+    nc = tc.nc
+    with ExitStack() as ctx:
+        const = ctx.enter_context(tc.tile_pool(name="const", bufs=1))
+        ctx.enter_context(tc.manual_schedule())
+        xpool = ctx.enter_context(tc.tile_pool(name="xpool", bufs=12))
+        net = ctx.enter_context(tc.tile_pool(name="net", bufs=4))
+        work = ctx.enter_context(tc.tile_pool(name="work", bufs=3))
+        small = ctx.enter_context(tc.tile_pool(name="small", bufs=2))
+        psx = ctx.enter_context(tc.psum_pool(name="psx", bufs=3))
+        psh = ctx.enter_context(tc.psum_pool(name="psh", bufs=4))
+        pso = ctx.enter_context(tc.psum_pool(name="pso", bufs=1))
+
+        w1raw = const.tile([P, 8, HID], BF16)
+        nc.sync.dma_start(
+            out=w1raw[:].rearrange("p (a e) h -> p a (e h)", e=2),
+            in_=W1.rearrange("(a p e) h -> p a (e h)", a=4, p=P, e=2),
+        )
+        xin = {}
+
+        def load(c):
+            b, kq = divmod(c, K // LPC)
+            xt_in = xpool.tile([P, LPC * IN], BF16, name="xin")
+            nc.sync.dma_start(
+                out=xt_in[:],
+                in_=net_in[b].rearrange("s k i -> s (k i)")[:, kq * LPC * IN:(kq + 1) * LPC * IN],
+            )
+            xin[c] = xt_in
+
+        load(0)
+        b1raw = const.tile([P, 4], BF16)
+        nc.scalar.dma_start(out=b1raw[:], in_=b1.rearrange("(q t) -> q t", t=4))
+        wfraw = const.tile([P, 4, CH], BF16)
+        nc.scalar.dma_start(out=wfraw[:].rearrange("p t c -> p (t c)"), in_=Wf.rearrange("(q t) c -> q (t c)", t=4))
+        load(1)
+        bfb = const.tile([P, CH], BF16)
+        nc.scalar.dma_start(out=bfb[:], in_=b_f.partition_broadcast(P))
+        msb = const.tile([P, B, K], BF16)
+        nc.scalar.dma_start(out=msb[:], in_=m.rearrange("b s k o -> s b (k o)"))
+        load(2)
+        emb = const.tile([P, B, CH], BF16)
+        nc.scalar.dma_start(out=emb[:, :, 0:OUT], in_=embeds.rearrange("b s c -> s b c"))
+        gmb = const.tile([P, CH], BF16)
+        nc.scalar.dma_start(out=gmb[:, 0:OUT], in_=gamma.partition_broadcast(P))
+        btb = const.tile([P, CH], BF16)
+        nc.scalar.dma_start(out=btb[:, 0:OUT], in_=beta.partition_broadcast(P))
+        for c in range(3, NCH):
+            load(c)
+
+        ident = const.tile([P, P], F32)
+        make_identity(nc, ident[:])
+        neghalf = const.tile([P, 1], F32)
+        nc.vector.memset(neghalf[:], -0.5)
+
+        w1g = const.tile([P, 2, HID, 4], BF16, align_bytes=64)
+        w1c = const.tile([P, 2, HID], U32, align_bytes=64)
+        w1s = const.tile([P, 2, HID], U8, align_bytes=64)
+        for g in range(2):
+            src = w1raw[:, 4 * g:4 * g + 4, :].rearrange("p j (q t) -> p t q j", t=4)
+            dst = w1g[:, g].rearrange("p (t q) j -> p t q j", t=4)
+            if g == 0:
+                nc.vector.tensor_copy(out=dst, in_=src)
+            else:
+                nc.scalar.copy(out=dst, in_=src)
+        b1f = const.tile([P, 4], F32)
+        nc.vector.tensor_copy(out=b1f[:], in_=b1raw[:])
+
+        def quantise_w1(g):
+            nc.vector.quantize_mx(
+                out=w1c[:, g, :].bitcast(FP8X4),
+                scales=w1s[:, g, :],
+                in_=w1g[:, g].rearrange("p h j -> p (h j)"),
+            )
+
+        quantise_w1(0)
+        wfg = const.tile([P, CH, 4], BF16, align_bytes=64)
+        nc.vector.tensor_copy(out=wfg[:], in_=wfraw[:].rearrange("p t c -> p c t"))
+        bf127 = const.tile([P, 1], F32)
+        nc.vector.tensor_copy(out=bf127[:], in_=bfb[:, OUT:CH])
+        mf = const.tile([P, B * K], F32)
+        nc.vector.tensor_copy(out=mf[:], in_=msb[:].rearrange("p b k -> p (b k)"))
+        wfc = const.tile([P, CH], U32, align_bytes=64)
+        wfs = const.tile([P, CH], U8, align_bytes=64)
+        nc.vector.quantize_mx(out=wfc[:].bitcast(FP8X4), scales=wfs[:], in_=wfg[:].rearrange("p c t -> p (c t)"))
+        quantise_w1(1)
+
+        sig = const.tile([P, B * K], F32)
+        gall = const.tile([P, B * K], F32)
+        sums_in = const.tile([P, B, 3, K], F32)
+
+        gnet, ncod, nsca, hpl, hgr, hcod, hsca, opb, acc = {}, {}, {}, {}, {}, {}, {}, {}, {}
+
+        def stage_a(c):
+            xf = xin[c][:].bitcast(F32)
+            gn = net.tile([P, 2, ROWS, 2], F32, name="gnet", align_bytes=64)
+            gnet[c] = gn
+            for g in range(2):
+                for lp in range(2):
+                    xt = psx.tile([P, 2, 2 * P], F32, name="xt")
+                    for u in range(2):
+                        for li in range(2):
+                            col = (2 * lp + li) * (IN // 2) + g * 256 + u * P
+                            nc.tensor.transpose(xt[:, u, li * P:(li + 1) * P], xf[:, col:col + P], ident[:])
+                    dst = gn[:, g, lp * 2 * P:(lp + 1) * 2 * P, :]
+                    src = xt[:].rearrange("p u r -> p r u")
+                    if c < LOOK and lp == 1:
+                        nc.vector.tensor_copy(out=dst, in_=src)
+                    else:
+                        nc.scalar.copy(out=dst, in_=src)
+
+        def stage_b(c):
+            nco = net.tile([P, 2, ROWS], U32, name="ncod", align_bytes=64)
+            nsc = net.tile([P, 2, ROWS], U8, name="nsca", align_bytes=64)
+            ncod[c], nsca[c] = nco, nsc
+            nc.vector.quantize_mx(
+                out=nco[:].rearrange("p g r -> p (g r)").bitcast(FP8X4),
+                scales=nsc[:].rearrange("p g r -> p (g r)"),
+                in_=gnet[c][:].rearrange("p g r u -> p (g r u)").bitcast(BF16),
+            )
+
+        def stage_c(c):
+            hp_sb = work.tile([P, 4, ROWS], BF16, name="hpl")
+            hpl[c] = hp_sb
+            for t in range(4):
+                hp = psh.tile([P, ROWS], F32, name="hp")
+                for g in range(2):
+                    nc.tensor.matmul_mx(
+                        out=hp[:],
+                        lhsT=w1c[:, g, t * P:(t + 1) * P].bitcast(FP8X4),
+                        lhsT_scale=w1s[:, g, t * P:(t + 1) * P],
+                        rhs=ncod[c][:, g, :].bitcast(FP8X4),
+                        rhs_scale=nsca[c][:, g, :],
+                        start=(g == 0),
+                        stop=(g == 1),
+                    )
+                if t == 3:
+                    nc.vector.tensor_scalar(out=hp_sb[:, t, :], in0=hp[:], scalar1=b1f[:, t:t + 1], scalar2=0.0,
+                                            op0=ALU.add, op1=ALU.max)
+                else:
+                    nc.scalar.activation(out=hp_sb[:, t, :], in_=hp[:], func=ACT.Relu, bias=b1f[:, t:t + 1], scale=1.0)
+
+        def stage_d(c):
+            hg = work.tile([P, ROWS, 4], BF16, name="hgr", align_bytes=64)
+            hgr[c] = hg
+            nc.vector.tensor_copy(
+                out=hg[:].rearrange("p (c i) t -> p c t i", i=4),
+                in_=hpl[c][:].rearrange("p t (c i) -> p c t i", i=4),
+            )
+
+        def stage_e(c):
+            hco = work.tile([P, ROWS], U32, name="hcod", align_bytes=64)
+            hsc = work.tile([P, ROWS], U8, name="hsca", align_bytes=64)
+            hcod[c], hsca[c] = hco, hsc
+            nc.vector.quantize_mx(out=hco[:].bitcast(FP8X4), scales=hsc[:], in_=hgr[c][:].rearrange("p r t -> p (r t)"))
+
+        def stage_f(c):
+            op = pso.tile([P, LPC, CH], F32, name="op")
+            opb[c] = op
+            for l in range(LPC):
+                nc.tensor.matmul_mx(
+                    out=op[:, l, :],
+                    lhsT=hcod[c][:, l * P:(l + 1) * P].bitcast(FP8X4),
+                    lhsT_scale=hsca[c][:, l * P:(l + 1) * P],
+                    rhs=wfc[:].bitcast(FP8X4),
+                    rhs_scale=wfs[:],
+                    start=True,
+                    stop=True,
+                )
+            cols = slice(c * LPC, (c + 1) * LPC)
+            nc.scalar.activation(out=sig[:, cols], in_=op[:, :, OUT], func=ACT.Sigmoid, bias=bf127[:, 0:1], scale=1.0)
+
+        def stage_gq(c):
+            b, kq = divmod(c, K // LPC)
+            cols = slice(c * LPC, (c + 1) * LPC)
+            ks = slice(kq * LPC, (kq + 1) * LPC)
+            if b < B - 1:
+                nc.gpsimd.tensor_tensor(out=gall[:, cols], in0=sig[:, cols], in1=mf[:, cols], op=ALU.mult)
+                nc.gpsimd.tensor_scalar_add(out=sums_in[:, b, 0, ks], in0=gall[:, cols], scalar1=LINK_EPS)
+                nc.gpsimd.tensor_tensor(out=sums_in[:, b, 2, ks], in0=sums_in[:, b, 0, ks], in1=mf[:, cols], op=ALU.mult)
+                nc.gpsimd.tensor_tensor(out=sums_in[:, b, 1, ks], in0=sums_in[:, b, 0, ks], in1=gall[:, cols], op=ALU.mult)
+            else:
+                nc.vector.tensor_tensor(out=gall[:, cols], in0=sig[:, cols], in1=mf[:, cols], op=ALU.mult)
+                nc.vector.scalar_tensor_tensor(out=sums_in[:, b, 2, ks], in0=gall[:, cols], scalar=LINK_EPS,
+                                               in1=mf[:, cols], op0=ALU.add, op1=ALU.mult)
+
+        def stage_stt(c):
+            b, kq = divmod(c, K // LPC)
+            op = opb[c]
+            if kq == 0:
+                acc_b = small.tile([P, 2, CH], F32, name="acc")
+                acc[b] = acc_b
+            a = acc[b]
+            for l in range(LPC):
+                qs = sums_in[:, b, 2, kq * LPC + l:kq * LPC + l + 1]
+                if kq == 0 and l < 2:
+                    nc.vector.tensor_scalar(out=a[:, l % 2, :], in0=op[:, l, :], scalar1=qs, scalar2=None, op0=ALU.mult)
+                else:
+                    nc.vector.scalar_tensor_tensor(out=a[:, l % 2, :], in0=op[:, l, :], scalar=qs, in1=a[:, l % 2, :],
+                                                   op0=ALU.mult, op1=ALU.add)
+
+        ln_y1, ln_rstd = {}, {}
+
+        def stage_ln1(b):
+            if b == B - 1:
+                g16 = gall[:, b * K:(b + 1) * K]
+                nc.vector.tensor_scalar_add(out=sums_in[:, b, 0, :], in0=g16, scalar1=LINK_EPS)
+                nc.vector.tensor_tensor(out=sums_in[:, b, 1, :], in0=sums_in[:, b, 0, :], in1=g16, op=ALU.mult)
+            sums = small.tile([P, 3], F32, name="sums")
+            nc.vector.tensor_reduce(out=sums[:], in_=sums_in[:, b], axis=AX.X, op=ALU.add)
+            rl = small.tile([P, 1], F32, name="rl")
+            nc.vector.reciprocal(out=rl[:], in_=sums[:, 0:1])
+            s12 = small.tile([P, 2], F32, name="s12")
+            nc.vector.tensor_scalar(out=s12[:, 0:1], in0=sums[:, 1:2], scalar1=rl[:, 0:1], scalar2=rl[:, 0:1],
+                                    op0=ALU.mult, op1=ALU.mult)
+            nc.vector.tensor_tensor(out=s12[:, 1:2], in0=s12[:, 0:1], in1=sums[:, 2:3], op=ALU.mult)
+            e0 = small.tile([P, OUT], F32, name="e0")
+            nc.vector.scalar_tensor_tensor(out=e0[:], in0=bfb[:, 0:OUT], scalar=s12[:, 1:2], in1=emb[:, b, 0:OUT],
+                                           op0=ALU.mult, op1=ALU.add)
+            e1 = small.tile([P, OUT], F32, name="e1")
+            nc.vector.scalar_tensor_tensor(out=e1[:], in0=acc[b][:, 0, 0:OUT], scalar=s12[:, 0:1], in1=e0[:],
+                                           op0=ALU.mult, op1=ALU.add)
+            e2 = small.tile([P, OUT], F32, name="e2")
+            nc.vector.scalar_tensor_tensor(out=e2[:], in0=acc[b][:, 1, 0:OUT], scalar=s12[:, 0:1], in1=e1[:],
+                                           op0=ALU.mult, op1=ALU.add)
+            st6 = small.tile([P, 6], F32, name="st6")
+            nc.vector.bn_stats(out=st6[:], in_=e2[:])
+            mv = small.tile([P, 2], F32, name="mv")
+            nc.vector.bn_aggr(out=mv[:], in_=st6[:])
+            vpe = small.tile([P, 1], F32, name="vpe")
+            nc.gpsimd.tensor_scalar_add(out=vpe[:], in0=mv[:, 1:2], scalar1=LN_EPS)
+            rstd = small.tile([P, 1], F32, name="rstd")
+            nc.gpsimd.tensor_tensor(out=rstd[:], in0=vpe[:], in1=neghalf[:], op=ALU.pow)
+            y1 = small.tile([P, OUT], F32, name="y1")
+            nc.vector.scalar_tensor_tensor(out=y1[:], in0=e2[:], scalar=mv[:, 0:1], in1=gmb[:, 0:OUT],
+                                           op0=ALU.subtract, op1=ALU.mult)
+            ln_y1[b], ln_rstd[b] = y1, rstd
+
+        def stage_ln2(b):
+            y2 = small.tile([P, OUT], F32, name="y2")
+            nc.vector.scalar_tensor_tensor(out=y2[:], in0=ln_y1[b][:], scalar=ln_rstd[b][:, 0:1], in1=btb[:, 0:OUT],
+                                           op0=ALU.mult, op1=ALU.add)
+            nc.sync.dma_start(out=out[b], in_=y2[:])
+
+        def on(c):
+            return 0 <= c < NCH
+
+        for c in range(LOOK):
+            stage_a(c)
+            stage_b(c)
+        for i in range(NCH + 2):
+            if on(i):
+                stage_c(i)
+            if on(i - 1):
+                stage_f(i - 1)
+            if on(i + LOOK):
+                stage_a(i + LOOK)
+            if on(i - 1):
+                stage_gq(i - 1)
+            if on(i):
+                stage_d(i)
+            last_of_batch = on(i - 1) and (i - 1) % (K // LPC) == K // LPC - 1
+            if on(i - 1):
+                stage_stt(i - 1)
+                if last_of_batch:
+                    stage_ln1((i - 1) // (K // LPC))
+            if on(i):
+                stage_e(i)
+            if on(i + LOOK):
+                stage_b(i + LOOK)
+            if last_of_batch:
+                stage_ln2((i - 1) // (K // LPC))

@@ -23,7 +23,11 @@ LINK_EPS = 1e-8
 
 FLOPS = 2 * B * S * K * IN * HID + 2 * B * S * K * HID * CH
 
-LOOK = 2
+PRE = 2
+T_AHEAD = 3
+Q_AHEAD = 2
+M2_LAG = 2
+V_BANK_CHUNKS = 6
 
 
 def tile_embed_update_pa_t_kernel(tc, net_in, embeds, m, W1, b1, Wf, b_f, gamma, beta, out):
@@ -32,12 +36,12 @@ def tile_embed_update_pa_t_kernel(tc, net_in, embeds, m, W1, b1, Wf, b_f, gamma,
         const = ctx.enter_context(tc.tile_pool(name="const", bufs=1))
         ctx.enter_context(tc.manual_schedule())
         xpool = ctx.enter_context(tc.tile_pool(name="xpool", bufs=12))
+        gpool = ctx.enter_context(tc.tile_pool(name="gpool", bufs=3))
         net = ctx.enter_context(tc.tile_pool(name="net", bufs=4))
         work = ctx.enter_context(tc.tile_pool(name="work", bufs=3))
         small = ctx.enter_context(tc.tile_pool(name="small", bufs=2))
-        psx = ctx.enter_context(tc.psum_pool(name="psx", bufs=3))
+        psx = ctx.enter_context(tc.psum_pool(name="psx", bufs=4))
         psh = ctx.enter_context(tc.psum_pool(name="psh", bufs=4))
-        pso = ctx.enter_context(tc.psum_pool(name="pso", bufs=1))
 
         w1raw = const.tile([P, 8, HID], BF16)
         nc.sync.dma_start(
@@ -118,23 +122,25 @@ def tile_embed_update_pa_t_kernel(tc, net_in, embeds, m, W1, b1, Wf, b_f, gamma,
 
         gnet, ncod, nsca, hpl, hgr, hcod, hsca, opb, acc = {}, {}, {}, {}, {}, {}, {}, {}, {}
 
-        def stage_a(c):
+        def stage_a(c, banks):
             xf = xin[c][:].bitcast(F32)
-            gn = net.tile([P, 2, ROWS, 2], F32, name="gnet", align_bytes=64)
-            gnet[c] = gn
-            for g in range(2):
-                for lp in range(2):
-                    xt = psx.tile([P, 2, 2 * P], F32, name="xt")
-                    for u in range(2):
-                        for li in range(2):
-                            col = (2 * lp + li) * (IN // 2) + g * 256 + u * P
-                            nc.tensor.transpose(xt[:, u, li * P:(li + 1) * P], xf[:, col:col + P], ident[:])
-                    dst = gn[:, g, lp * 2 * P:(lp + 1) * 2 * P, :]
-                    src = xt[:].rearrange("p u r -> p r u")
-                    if c < LOOK and lp == 1:
-                        nc.vector.tensor_copy(out=dst, in_=src)
-                    else:
-                        nc.scalar.copy(out=dst, in_=src)
+            if c not in gnet:
+                gn_new = gpool.tile([P, 2, ROWS, 2], F32, name="gnet", align_bytes=64)
+                gnet[c] = gn_new
+            gn = gnet[c]
+            for j in banks:
+                g, lp = divmod(j, 2)
+                xt = psx.tile([P, 2, 2 * P], F32, name="xt", tag="xo")
+                for u in range(2):
+                    for li in range(2):
+                        col = (2 * lp + li) * (IN // 2) + g * 256 + u * P
+                        nc.tensor.transpose(xt[:, u, li * P:(li + 1) * P], xf[:, col:col + P], ident[:])
+                dst = gn[:, g, lp * 2 * P:(lp + 1) * 2 * P, :]
+                src = xt[:].rearrange("p u r -> p r u")
+                if c < PRE and lp == 1:
+                    nc.vector.tensor_copy(out=dst, in_=src)
+                else:
+                    nc.scalar.copy(out=dst, in_=src)
 
         def stage_b(c):
             nco = net.tile([P, 2, ROWS], U32, name="ncod", align_bytes=64)
@@ -146,10 +152,13 @@ def tile_embed_update_pa_t_kernel(tc, net_in, embeds, m, W1, b1, Wf, b_f, gamma,
                 in_=gnet[c][:].rearrange("p g r u -> p (g r u)").bitcast(BF16),
             )
 
-        def stage_c(c):
-            hp_sb = work.tile([P, 4, ROWS], BF16, name="hpl")
-            hpl[c] = hp_sb
-            for t in range(4):
+        hbank = {}
+
+        def stage_c(c, blocks):
+            if c not in hpl:
+                hp_new = work.tile([P, 4, ROWS], BF16, name="hpl")
+                hpl[c] = hp_new
+            for t in blocks:
                 hp = psh.tile([P, ROWS], F32, name="hp")
                 for g in range(2):
                     nc.tensor.matmul_mx(
@@ -161,11 +170,14 @@ def tile_embed_update_pa_t_kernel(tc, net_in, embeds, m, W1, b1, Wf, b_f, gamma,
                         start=(g == 0),
                         stop=(g == 1),
                     )
-                if t == 3:
-                    nc.vector.tensor_scalar(out=hp_sb[:, t, :], in0=hp[:], scalar1=b1f[:, t:t + 1], scalar2=0.0,
-                                            op0=ALU.add, op1=ALU.max)
+                if t == 0 and c < V_BANK_CHUNKS:
+                    hbank[c] = hp
                 else:
-                    nc.scalar.activation(out=hp_sb[:, t, :], in_=hp[:], func=ACT.Relu, bias=b1f[:, t:t + 1], scale=1.0)
+                    nc.scalar.activation(out=hpl[c][:, t, :], in_=hp[:], func=ACT.Relu, bias=b1f[:, t:t + 1], scale=1.0)
+
+        def stage_cv(c):
+            nc.vector.tensor_scalar(out=hpl[c][:, 0, :], in0=hbank[c][:], scalar1=b1f[:, 0:1], scalar2=0.0,
+                                    op0=ALU.add, op1=ALU.max)
 
         def stage_d(c):
             hg = work.tile([P, ROWS, 4], BF16, name="hgr", align_bytes=64)
@@ -182,7 +194,7 @@ def tile_embed_update_pa_t_kernel(tc, net_in, embeds, m, W1, b1, Wf, b_f, gamma,
             nc.vector.quantize_mx(out=hco[:].bitcast(FP8X4), scales=hsc[:], in_=hgr[c][:].rearrange("p r t -> p (r t)"))
 
         def stage_f(c):
-            op = pso.tile([P, LPC, CH], F32, name="op")
+            op = psx.tile([P, LPC, CH], F32, name="op", tag="xo")
             opb[c] = op
             for l in range(LPC):
                 nc.tensor.matmul_mx(
@@ -201,15 +213,9 @@ def tile_embed_update_pa_t_kernel(tc, net_in, embeds, m, W1, b1, Wf, b_f, gamma,
             b, kq = divmod(c, K // LPC)
             cols = slice(c * LPC, (c + 1) * LPC)
             ks = slice(kq * LPC, (kq + 1) * LPC)
-            if b < B - 1:
-                nc.gpsimd.tensor_tensor(out=gall[:, cols], in0=sig[:, cols], in1=mf[:, cols], op=ALU.mult)
-                nc.gpsimd.tensor_scalar_add(out=sums_in[:, b, 0, ks], in0=gall[:, cols], scalar1=LINK_EPS)
-                nc.gpsimd.tensor_tensor(out=sums_in[:, b, 2, ks], in0=sums_in[:, b, 0, ks], in1=mf[:, cols], op=ALU.mult)
-                nc.gpsimd.tensor_tensor(out=sums_in[:, b, 1, ks], in0=sums_in[:, b, 0, ks], in1=gall[:, cols], op=ALU.mult)
-            else:
-                nc.vector.tensor_tensor(out=gall[:, cols], in0=sig[:, cols], in1=mf[:, cols], op=ALU.mult)
-                nc.vector.scalar_tensor_tensor(out=sums_in[:, b, 2, ks], in0=gall[:, cols], scalar=LINK_EPS,
-                                               in1=mf[:, cols], op0=ALU.add, op1=ALU.mult)
+            nc.vector.tensor_tensor(out=gall[:, cols], in0=sig[:, cols], in1=mf[:, cols], op=ALU.mult)
+            nc.vector.scalar_tensor_tensor(out=sums_in[:, b, 2, ks], in0=gall[:, cols], scalar=LINK_EPS,
+                                           in1=mf[:, cols], op0=ALU.add, op1=ALU.mult)
 
         def stage_stt(c):
             b, kq = divmod(c, K // LPC)
@@ -229,10 +235,9 @@ def tile_embed_update_pa_t_kernel(tc, net_in, embeds, m, W1, b1, Wf, b_f, gamma,
         ln_y1, ln_rstd = {}, {}
 
         def stage_ln1(b):
-            if b == B - 1:
-                g16 = gall[:, b * K:(b + 1) * K]
-                nc.vector.tensor_scalar_add(out=sums_in[:, b, 0, :], in0=g16, scalar1=LINK_EPS)
-                nc.vector.tensor_tensor(out=sums_in[:, b, 1, :], in0=sums_in[:, b, 0, :], in1=g16, op=ALU.mult)
+            g16 = gall[:, b * K:(b + 1) * K]
+            nc.vector.tensor_scalar_add(out=sums_in[:, b, 0, :], in0=g16, scalar1=LINK_EPS)
+            nc.vector.tensor_tensor(out=sums_in[:, b, 1, :], in0=sums_in[:, b, 0, :], in1=g16, op=ALU.mult)
             sums = small.tile([P, 3], F32, name="sums")
             nc.vector.tensor_reduce(out=sums[:], in_=sums_in[:, b], axis=AX.X, op=ALU.add)
             rl = small.tile([P, 1], F32, name="rl")
@@ -272,28 +277,41 @@ def tile_embed_update_pa_t_kernel(tc, net_in, embeds, m, W1, b1, Wf, b_f, gamma,
         def on(c):
             return 0 <= c < NCH
 
-        for c in range(LOOK):
-            stage_a(c)
+        for c in range(PRE):
+            stage_a(c, (0, 1, 2, 3))
             stage_b(c)
-        for i in range(NCH + 2):
-            if on(i):
-                stage_c(i)
+        next_t = PRE
+        pending_ln = []
+        cpb = K // LPC
+        for i in range(NCH + M2_LAG + 2):
+            ahead = []
+            while next_t < NCH and next_t <= i + T_AHEAD:
+                ahead.append(next_t)
+                next_t += 1
+            for half in ((0, 1), (2, 3)):
+                if on(i):
+                    stage_c(i, half)
+                for c in ahead:
+                    stage_a(c, half)
+            if on(i - M2_LAG):
+                stage_f(i - M2_LAG)
+            j = i - M2_LAG - 1
+            if on(j):
+                stage_gq(j)
+                stage_stt(j)
+            for b in pending_ln:
+                stage_ln2(b)
+            pending_ln = []
+            if on(j) and j % cpb == cpb - 1:
+                stage_ln1(j // cpb)
+                pending_ln.append(j // cpb)
             if on(i - 1):
-                stage_f(i - 1)
-            if on(i + LOOK):
-                stage_a(i + LOOK)
+                stage_d(i - 1)
+            if on(i) and i < V_BANK_CHUNKS:
+                stage_cv(i)
+            if PRE <= i + Q_AHEAD < NCH:
+                stage_b(i + Q_AHEAD)
             if on(i - 1):
-                stage_gq(i - 1)
-            if on(i):
-                stage_d(i)
-            last_of_batch = on(i - 1) and (i - 1) % (K // LPC) == K // LPC - 1
-            if on(i - 1):
-                stage_stt(i - 1)
-                if last_of_batch:
-                    stage_ln1((i - 1) // (K // LPC))
-            if on(i):
-                stage_e(i)
-            if on(i + LOOK):
-                stage_b(i + LOOK)
-            if last_of_batch:
-                stage_ln2((i - 1) // (K // LPC))
+                stage_e(i - 1)
+        for b in pending_ln:
+            stage_ln2(b)

@@ -23,25 +23,20 @@ LINK_EPS = 1e-8
 
 FLOPS = 2 * B * S * K * IN * HID + 2 * B * S * K * HID * CH
 
-PRE = 2
-T_AHEAD = 3
-Q_AHEAD = 2
-M2_LAG = 2
-V_BANK_CHUNKS = 6
+V_XT = ((3, 1),)
+V_HP = ()
 
 
 def tile_embed_update_pa_t_kernel(tc, net_in, embeds, m, W1, b1, Wf, b_f, gamma, beta, out):
     nc = tc.nc
     with ExitStack() as ctx:
         const = ctx.enter_context(tc.tile_pool(name="const", bufs=1))
-        ctx.enter_context(tc.manual_schedule())
-        xpool = ctx.enter_context(tc.tile_pool(name="xpool", bufs=12))
-        gpool = ctx.enter_context(tc.tile_pool(name="gpool", bufs=3))
-        net = ctx.enter_context(tc.tile_pool(name="net", bufs=4))
+        xpool = ctx.enter_context(tc.tile_pool(name="xpool", bufs=8))
         work = ctx.enter_context(tc.tile_pool(name="work", bufs=3))
         small = ctx.enter_context(tc.tile_pool(name="small", bufs=2))
-        psx = ctx.enter_context(tc.psum_pool(name="psx", bufs=4))
+        psx = ctx.enter_context(tc.psum_pool(name="psx", bufs=3))
         psh = ctx.enter_context(tc.psum_pool(name="psh", bufs=4))
+        pso = ctx.enter_context(tc.psum_pool(name="pso", bufs=1))
 
         w1raw = const.tile([P, 8, HID], BF16)
         nc.sync.dma_start(
@@ -96,15 +91,12 @@ def tile_embed_update_pa_t_kernel(tc, net_in, embeds, m, W1, b1, Wf, b_f, gamma,
                 nc.scalar.copy(out=dst, in_=src)
         b1f = const.tile([P, 4], F32)
         nc.vector.tensor_copy(out=b1f[:], in_=b1raw[:])
-
-        def quantise_w1(g):
+        for g in range(2):
             nc.vector.quantize_mx(
                 out=w1c[:, g, :].bitcast(FP8X4),
                 scales=w1s[:, g, :],
                 in_=w1g[:, g].rearrange("p h j -> p (h j)"),
             )
-
-        quantise_w1(0)
         wfg = const.tile([P, CH, 4], BF16, align_bytes=64)
         nc.vector.tensor_copy(out=wfg[:], in_=wfraw[:].rearrange("p t c -> p c t"))
         bf127 = const.tile([P, 1], F32)
@@ -114,7 +106,6 @@ def tile_embed_update_pa_t_kernel(tc, net_in, embeds, m, W1, b1, Wf, b_f, gamma,
         wfc = const.tile([P, CH], U32, align_bytes=64)
         wfs = const.tile([P, CH], U8, align_bytes=64)
         nc.vector.quantize_mx(out=wfc[:].bitcast(FP8X4), scales=wfs[:], in_=wfg[:].rearrange("p c t -> p (c t)"))
-        quantise_w1(1)
 
         sig = const.tile([P, B * K], F32)
         gall = const.tile([P, B * K], F32)
@@ -122,29 +113,27 @@ def tile_embed_update_pa_t_kernel(tc, net_in, embeds, m, W1, b1, Wf, b_f, gamma,
 
         gnet, ncod, nsca, hpl, hgr, hcod, hsca, opb, acc = {}, {}, {}, {}, {}, {}, {}, {}, {}
 
-        def stage_a(c, banks):
+        def stage_a(c):
             xf = xin[c][:].bitcast(F32)
-            if c not in gnet:
-                gn_new = gpool.tile([P, 2, ROWS, 2], F32, name="gnet", align_bytes=64)
-                gnet[c] = gn_new
-            gn = gnet[c]
-            for j in banks:
-                g, lp = divmod(j, 2)
-                xt = psx.tile([P, 2, 2 * P], F32, name="xt", tag="xo")
-                for u in range(2):
-                    for li in range(2):
-                        col = (2 * lp + li) * (IN // 2) + g * 256 + u * P
-                        nc.tensor.transpose(xt[:, u, li * P:(li + 1) * P], xf[:, col:col + P], ident[:])
-                dst = gn[:, g, lp * 2 * P:(lp + 1) * 2 * P, :]
-                src = xt[:].rearrange("p u r -> p r u")
-                if c < PRE and lp == 1:
-                    nc.vector.tensor_copy(out=dst, in_=src)
-                else:
-                    nc.scalar.copy(out=dst, in_=src)
+            gn = work.tile([P, 2, ROWS, 2], F32, name="gnet", align_bytes=64)
+            gnet[c] = gn
+            for g in range(2):
+                for lp in range(2):
+                    xt = psx.tile([P, 2, 2 * P], F32, name="xt")
+                    for u in range(2):
+                        for li in range(2):
+                            col = (2 * lp + li) * (IN // 2) + g * 256 + u * P
+                            nc.tensor.transpose(xt[:, u, li * P:(li + 1) * P], xf[:, col:col + P], ident[:])
+                    dst = gn[:, g, lp * 2 * P:(lp + 1) * 2 * P, :]
+                    src = xt[:].rearrange("p u r -> p r u")
+                    if (2 * g + lp, c % 2) in V_XT:
+                        nc.vector.tensor_copy(out=dst, in_=src)
+                    else:
+                        nc.scalar.copy(out=dst, in_=src)
 
         def stage_b(c):
-            nco = net.tile([P, 2, ROWS], U32, name="ncod", align_bytes=64)
-            nsc = net.tile([P, 2, ROWS], U8, name="nsca", align_bytes=64)
+            nco = work.tile([P, 2, ROWS], U32, name="ncod", align_bytes=64)
+            nsc = work.tile([P, 2, ROWS], U8, name="nsca", align_bytes=64)
             ncod[c], nsca[c] = nco, nsc
             nc.vector.quantize_mx(
                 out=nco[:].rearrange("p g r -> p (g r)").bitcast(FP8X4),
@@ -152,13 +141,10 @@ def tile_embed_update_pa_t_kernel(tc, net_in, embeds, m, W1, b1, Wf, b_f, gamma,
                 in_=gnet[c][:].rearrange("p g r u -> p (g r u)").bitcast(BF16),
             )
 
-        hbank = {}
-
-        def stage_c(c, blocks):
-            if c not in hpl:
-                hp_new = work.tile([P, 4, ROWS], BF16, name="hpl")
-                hpl[c] = hp_new
-            for t in blocks:
+        def stage_c(c):
+            hp_sb = work.tile([P, 4, ROWS], BF16, name="hpl")
+            hpl[c] = hp_sb
+            for t in range(4):
                 hp = psh.tile([P, ROWS], F32, name="hp")
                 for g in range(2):
                     nc.tensor.matmul_mx(
@@ -170,14 +156,11 @@ def tile_embed_update_pa_t_kernel(tc, net_in, embeds, m, W1, b1, Wf, b_f, gamma,
                         start=(g == 0),
                         stop=(g == 1),
                     )
-                if t == 0 and c < V_BANK_CHUNKS:
-                    hbank[c] = hp
+                if (t, c % 2) in V_HP:
+                    nc.vector.tensor_scalar(out=hp_sb[:, t, :], in0=hp[:], scalar1=b1f[:, t:t + 1], scalar2=0.0,
+                                            op0=ALU.add, op1=ALU.max)
                 else:
-                    nc.scalar.activation(out=hpl[c][:, t, :], in_=hp[:], func=ACT.Relu, bias=b1f[:, t:t + 1], scale=1.0)
-
-        def stage_cv(c):
-            nc.vector.tensor_scalar(out=hpl[c][:, 0, :], in0=hbank[c][:], scalar1=b1f[:, 0:1], scalar2=0.0,
-                                    op0=ALU.add, op1=ALU.max)
+                    nc.scalar.activation(out=hp_sb[:, t, :], in_=hp[:], func=ACT.Relu, bias=b1f[:, t:t + 1], scale=1.0)
 
         def stage_d(c):
             hg = work.tile([P, ROWS, 4], BF16, name="hgr", align_bytes=64)
@@ -194,7 +177,7 @@ def tile_embed_update_pa_t_kernel(tc, net_in, embeds, m, W1, b1, Wf, b_f, gamma,
             nc.vector.quantize_mx(out=hco[:].bitcast(FP8X4), scales=hsc[:], in_=hgr[c][:].rearrange("p r t -> p (r t)"))
 
         def stage_f(c):
-            op = psx.tile([P, LPC, CH], F32, name="op", tag="xo")
+            op = pso.tile([P, LPC, CH], F32, name="op")
             opb[c] = op
             for l in range(LPC):
                 nc.tensor.matmul_mx(
@@ -209,17 +192,14 @@ def tile_embed_update_pa_t_kernel(tc, net_in, embeds, m, W1, b1, Wf, b_f, gamma,
             cols = slice(c * LPC, (c + 1) * LPC)
             nc.scalar.activation(out=sig[:, cols], in_=op[:, :, OUT], func=ACT.Sigmoid, bias=bf127[:, 0:1], scale=1.0)
 
-        def stage_gq(c):
-            b, kq = divmod(c, K // LPC)
-            cols = slice(c * LPC, (c + 1) * LPC)
-            ks = slice(kq * LPC, (kq + 1) * LPC)
-            nc.vector.tensor_tensor(out=gall[:, cols], in0=sig[:, cols], in1=mf[:, cols], op=ALU.mult)
-            nc.vector.scalar_tensor_tensor(out=sums_in[:, b, 2, ks], in0=gall[:, cols], scalar=LINK_EPS,
-                                           in1=mf[:, cols], op0=ALU.add, op1=ALU.mult)
-
-        def stage_stt(c):
+        def stage_g(c):
             b, kq = divmod(c, K // LPC)
             op = opb[c]
+            cols = slice(c * LPC, (c + 1) * LPC)
+            q = sums_in[:, b, 2, kq * LPC:(kq + 1) * LPC]
+            nc.vector.tensor_tensor(out=gall[:, cols], in0=sig[:, cols], in1=mf[:, cols], op=ALU.mult)
+            nc.vector.scalar_tensor_tensor(out=q, in0=gall[:, cols], scalar=LINK_EPS, in1=mf[:, cols],
+                                           op0=ALU.add, op1=ALU.mult)
             if kq == 0:
                 acc_b = small.tile([P, 2, CH], F32, name="acc")
                 acc[b] = acc_b
@@ -232,9 +212,7 @@ def tile_embed_update_pa_t_kernel(tc, net_in, embeds, m, W1, b1, Wf, b_f, gamma,
                     nc.vector.scalar_tensor_tensor(out=a[:, l % 2, :], in0=op[:, l, :], scalar=qs, in1=a[:, l % 2, :],
                                                    op0=ALU.mult, op1=ALU.add)
 
-        ln_y1, ln_rstd = {}, {}
-
-        def stage_ln1(b):
+        def stage_ln(b):
             g16 = gall[:, b * K:(b + 1) * K]
             nc.vector.tensor_scalar_add(out=sums_in[:, b, 0, :], in0=g16, scalar1=LINK_EPS)
             nc.vector.tensor_tensor(out=sums_in[:, b, 1, :], in0=sums_in[:, b, 0, :], in1=g16, op=ALU.mult)
@@ -266,52 +244,30 @@ def tile_embed_update_pa_t_kernel(tc, net_in, embeds, m, W1, b1, Wf, b_f, gamma,
             y1 = small.tile([P, OUT], F32, name="y1")
             nc.vector.scalar_tensor_tensor(out=y1[:], in0=e2[:], scalar=mv[:, 0:1], in1=gmb[:, 0:OUT],
                                            op0=ALU.subtract, op1=ALU.mult)
-            ln_y1[b], ln_rstd[b] = y1, rstd
-
-        def stage_ln2(b):
             y2 = small.tile([P, OUT], F32, name="y2")
-            nc.vector.scalar_tensor_tensor(out=y2[:], in0=ln_y1[b][:], scalar=ln_rstd[b][:, 0:1], in1=btb[:, 0:OUT],
+            nc.vector.scalar_tensor_tensor(out=y2[:], in0=y1[:], scalar=rstd[:, 0:1], in1=btb[:, 0:OUT],
                                            op0=ALU.mult, op1=ALU.add)
             nc.sync.dma_start(out=out[b], in_=y2[:])
 
         def on(c):
             return 0 <= c < NCH
 
-        for c in range(PRE):
-            stage_a(c, (0, 1, 2, 3))
-            stage_b(c)
-        next_t = PRE
-        pending_ln = []
-        cpb = K // LPC
-        for i in range(NCH + M2_LAG + 2):
-            ahead = []
-            while next_t < NCH and next_t <= i + T_AHEAD:
-                ahead.append(next_t)
-                next_t += 1
-            for half in ((0, 1), (2, 3)):
-                if on(i):
-                    stage_c(i, half)
-                for c in ahead:
-                    stage_a(c, half)
-            if on(i - M2_LAG):
-                stage_f(i - M2_LAG)
-            j = i - M2_LAG - 1
-            if on(j):
-                stage_gq(j)
-                stage_stt(j)
-            for b in pending_ln:
-                stage_ln2(b)
-            pending_ln = []
-            if on(j) and j % cpb == cpb - 1:
-                stage_ln1(j // cpb)
-                pending_ln.append(j // cpb)
+        stage_a(0)
+        stage_b(0)
+        for i in range(NCH + 3):
+            if on(i + 1):
+                stage_a(i + 1)
+            if on(i):
+                stage_c(i)
             if on(i - 1):
                 stage_d(i - 1)
-            if on(i) and i < V_BANK_CHUNKS:
-                stage_cv(i)
-            if PRE <= i + Q_AHEAD < NCH:
-                stage_b(i + Q_AHEAD)
+            if on(i - 2):
+                stage_g(i - 2)
+                if (i - 2) % (K // LPC) == K // LPC - 1:
+                    stage_ln((i - 2) // (K // LPC))
             if on(i - 1):
                 stage_e(i - 1)
-        for b in pending_ln:
-            stage_ln2(b)
+            if on(i + 1):
+                stage_b(i + 1)
+            if on(i - 1):
+                stage_f(i - 1)

@@ -23,26 +23,22 @@ LINK_EPS = 1e-8
 
 FLOPS = 2 * B * S * K * IN * HID + 2 * B * S * K * HID * CH
 
-V_XT = ((3, 1),)
-V_HP = ()
+UNIT_LAG = 2
+M2_LAG = 2
+S_REGROUP_FROM = 3
 
 
 def tile_embed_update_pa_t_kernel(tc, net_in, embeds, m, W1, b1, Wf, b_f, gamma, beta, out):
     nc = tc.nc
     with ExitStack() as ctx:
         const = ctx.enter_context(tc.tile_pool(name="const", bufs=1))
-        xpool = ctx.enter_context(tc.tile_pool(name="xpool", bufs=8))
+        xpool = ctx.enter_context(tc.tile_pool(name="xpool", bufs=5))
+        gpool = ctx.enter_context(tc.tile_pool(name="gpool", bufs=3))
+        net = ctx.enter_context(tc.tile_pool(name="net", bufs=14))
         work = ctx.enter_context(tc.tile_pool(name="work", bufs=3))
         small = ctx.enter_context(tc.tile_pool(name="small", bufs=2))
-        psx = ctx.enter_context(tc.psum_pool(name="psx", bufs=3))
-        psh = ctx.enter_context(tc.psum_pool(name="psh", bufs=4))
-        pso = ctx.enter_context(tc.psum_pool(name="pso", bufs=1))
+        psum = ctx.enter_context(tc.psum_pool(name="psum", bufs=8))
 
-        w1raw = const.tile([P, 8, HID], BF16)
-        nc.sync.dma_start(
-            out=w1raw[:].rearrange("p (a e) h -> p a (e h)", e=2),
-            in_=W1.rearrange("(a p e) h -> p a (e h)", a=4, p=P, e=2),
-        )
         xin = {}
 
         def load(c):
@@ -55,57 +51,73 @@ def tile_embed_update_pa_t_kernel(tc, net_in, embeds, m, W1, b1, Wf, b_f, gamma,
             xin[c] = xt_in
 
         load(0)
+        w1raw = const.tile([P, 8, HID], BF16)
+        nc.sync.dma_start(
+            out=w1raw[:].rearrange("p (a e) h -> p a (e h)", e=2),
+            in_=W1.rearrange("(a p e) h -> p a (e h)", a=4, p=P, e=2),
+        )
         b1raw = const.tile([P, 4], BF16)
         nc.scalar.dma_start(out=b1raw[:], in_=b1.rearrange("(q t) -> q t", t=4))
         wfraw = const.tile([P, 4, CH], BF16)
         nc.scalar.dma_start(out=wfraw[:].rearrange("p t c -> p (t c)"), in_=Wf.rearrange("(q t) c -> q (t c)", t=4))
-        load(1)
-        bfb = const.tile([P, CH], BF16)
-        nc.scalar.dma_start(out=bfb[:], in_=b_f.partition_broadcast(P))
+        rows3 = const.tile([P, 4, CH], BF16)
+        nc.vector.memset(rows3[:], 0.0)
+        nc.scalar.dma_start(out=rows3[0:1, 0, :], in_=b_f.unsqueeze(0))
+        nc.scalar.dma_start(out=rows3[0:1, 1, 0:OUT], in_=gamma.unsqueeze(0))
+        nc.scalar.dma_start(out=rows3[0:1, 2, 0:OUT], in_=beta.unsqueeze(0))
         msb = const.tile([P, B, K], BF16)
         nc.scalar.dma_start(out=msb[:], in_=m.rearrange("b s k o -> s b (k o)"))
-        load(2)
         emb = const.tile([P, B, CH], BF16)
         nc.scalar.dma_start(out=emb[:, :, 0:OUT], in_=embeds.rearrange("b s c -> s b c"))
-        gmb = const.tile([P, CH], BF16)
-        nc.scalar.dma_start(out=gmb[:, 0:OUT], in_=gamma.partition_broadcast(P))
-        btb = const.tile([P, CH], BF16)
-        nc.scalar.dma_start(out=btb[:, 0:OUT], in_=beta.partition_broadcast(P))
-        for c in range(3, NCH):
+        for c in range(1, NCH):
             load(c)
 
         ident = const.tile([P, P], F32)
         make_identity(nc, ident[:])
         neghalf = const.tile([P, 1], F32)
         nc.vector.memset(neghalf[:], -0.5)
+        ones = const.tile([P, P], BF16)
+        nc.vector.memset(ones[:], 1.0)
+        spread_ps = psum.tile([P, 4, CH], F32, name="spread_ps", tag="bank")
+        nc.tensor.matmul(out=spread_ps[:], lhsT=ones[:], rhs=rows3[:], start=True, stop=True)
+        spread = const.tile([P, 3, CH], F32)
+        nc.vector.tensor_copy(out=spread[:], in_=spread_ps[:, 0:3, :])
+        bfb = spread[:, 0, :]
+        gmb = spread[:, 1, :]
+        btb = spread[:, 2, :]
 
         w1g = const.tile([P, 2, HID, 4], BF16, align_bytes=64)
         w1c = const.tile([P, 2, HID], U32, align_bytes=64)
         w1s = const.tile([P, 2, HID], U8, align_bytes=64)
-        for g in range(2):
-            src = w1raw[:, 4 * g:4 * g + 4, :].rearrange("p j (q t) -> p t q j", t=4)
-            dst = w1g[:, g].rearrange("p (t q) j -> p t q j", t=4)
-            if g == 0:
-                nc.vector.tensor_copy(out=dst, in_=src)
-            else:
-                nc.scalar.copy(out=dst, in_=src)
         b1f = const.tile([P, 4], F32)
-        nc.vector.tensor_copy(out=b1f[:], in_=b1raw[:])
-        for g in range(2):
+        wfg = const.tile([P, CH, 4], BF16, align_bytes=64)
+        bf127 = const.tile([P, 1], F32)
+        mf = const.tile([P, B * K], F32)
+        wfc = const.tile([P, CH], U32, align_bytes=64)
+        wfs = const.tile([P, CH], U8, align_bytes=64)
+
+        def quantise_w1(g):
             nc.vector.quantize_mx(
                 out=w1c[:, g, :].bitcast(FP8X4),
                 scales=w1s[:, g, :],
                 in_=w1g[:, g].rearrange("p h j -> p (h j)"),
             )
-        wfg = const.tile([P, CH, 4], BF16, align_bytes=64)
-        nc.vector.tensor_copy(out=wfg[:], in_=wfraw[:].rearrange("p t c -> p c t"))
-        bf127 = const.tile([P, 1], F32)
-        nc.vector.tensor_copy(out=bf127[:], in_=bfb[:, OUT:CH])
-        mf = const.tile([P, B * K], F32)
-        nc.vector.tensor_copy(out=mf[:], in_=msb[:].rearrange("p b k -> p (b k)"))
-        wfc = const.tile([P, CH], U32, align_bytes=64)
-        wfs = const.tile([P, CH], U8, align_bytes=64)
-        nc.vector.quantize_mx(out=wfc[:].bitcast(FP8X4), scales=wfs[:], in_=wfg[:].rearrange("p c t -> p (c t)"))
+
+        def prepare_weights():
+            for g in range(2):
+                src = w1raw[:, 4 * g:4 * g + 4, :].rearrange("p j (q t) -> p t q j", t=4)
+                dst = w1g[:, g].rearrange("p (t q) j -> p t q j", t=4)
+                if g == 0:
+                    nc.vector.tensor_copy(out=dst, in_=src)
+                else:
+                    nc.scalar.copy(out=dst, in_=src)
+            nc.vector.tensor_copy(out=b1f[:], in_=b1raw[:])
+            quantise_w1(0)
+            nc.vector.tensor_copy(out=wfg[:], in_=wfraw[:].rearrange("p t c -> p c t"))
+            nc.vector.tensor_copy(out=bf127[:], in_=bfb[:, OUT:CH])
+            nc.vector.tensor_copy(out=mf[:], in_=msb[:].rearrange("p b k -> p (b k)"))
+            nc.vector.quantize_mx(out=wfc[:].bitcast(FP8X4), scales=wfs[:], in_=wfg[:].rearrange("p c t -> p (c t)"))
+            quantise_w1(1)
 
         sig = const.tile([P, B * K], F32)
         gall = const.tile([P, B * K], F32)
@@ -113,27 +125,29 @@ def tile_embed_update_pa_t_kernel(tc, net_in, embeds, m, W1, b1, Wf, b_f, gamma,
 
         gnet, ncod, nsca, hpl, hgr, hcod, hsca, opb, acc = {}, {}, {}, {}, {}, {}, {}, {}, {}
 
-        def stage_a(c):
+        def stage_a(c, banks):
             xf = xin[c][:].bitcast(F32)
-            gn = work.tile([P, 2, ROWS, 2], F32, name="gnet", align_bytes=64)
-            gnet[c] = gn
-            for g in range(2):
-                for lp in range(2):
-                    xt = psx.tile([P, 2, 2 * P], F32, name="xt")
-                    for u in range(2):
-                        for li in range(2):
-                            col = (2 * lp + li) * (IN // 2) + g * 256 + u * P
-                            nc.tensor.transpose(xt[:, u, li * P:(li + 1) * P], xf[:, col:col + P], ident[:])
-                    dst = gn[:, g, lp * 2 * P:(lp + 1) * 2 * P, :]
-                    src = xt[:].rearrange("p u r -> p r u")
-                    if (2 * g + lp, c % 2) in V_XT:
-                        nc.vector.tensor_copy(out=dst, in_=src)
-                    else:
-                        nc.scalar.copy(out=dst, in_=src)
+            if c not in gnet:
+                gn_new = gpool.tile([P, 2, ROWS, 2], F32, name="gnet", align_bytes=64)
+                gnet[c] = gn_new
+            gn = gnet[c]
+            for j in banks:
+                g, lp = divmod(j, 2)
+                xt = psum.tile([P, 2, 2 * P], F32, name="xt", tag="bank")
+                for u in range(2):
+                    for li in range(2):
+                        col = (2 * lp + li) * (IN // 2) + g * 256 + u * P
+                        nc.tensor.transpose(xt[:, u, li * P:(li + 1) * P], xf[:, col:col + P], ident[:])
+                dst = gn[:, g, lp * 2 * P:(lp + 1) * 2 * P, :]
+                src = xt[:].rearrange("p u r -> p r u")
+                if j == 3:
+                    nc.vector.tensor_copy(out=dst, in_=src)
+                else:
+                    nc.scalar.copy(out=dst, in_=src)
 
         def stage_b(c):
-            nco = work.tile([P, 2, ROWS], U32, name="ncod", align_bytes=64)
-            nsc = work.tile([P, 2, ROWS], U8, name="nsca", align_bytes=64)
+            nco = net.tile([P, 2, ROWS], U32, name="ncod", align_bytes=64)
+            nsc = net.tile([P, 2, ROWS], U8, name="nsca", align_bytes=64)
             ncod[c], nsca[c] = nco, nsc
             nc.vector.quantize_mx(
                 out=nco[:].rearrange("p g r -> p (g r)").bitcast(FP8X4),
@@ -141,11 +155,12 @@ def tile_embed_update_pa_t_kernel(tc, net_in, embeds, m, W1, b1, Wf, b_f, gamma,
                 in_=gnet[c][:].rearrange("p g r u -> p (g r u)").bitcast(BF16),
             )
 
-        def stage_c(c):
-            hp_sb = work.tile([P, 4, ROWS], BF16, name="hpl")
-            hpl[c] = hp_sb
-            for t in range(4):
-                hp = psh.tile([P, ROWS], F32, name="hp")
+        def stage_c(c, blocks):
+            if c not in hpl:
+                hp_new = work.tile([P, 4, ROWS], BF16, name="hpl")
+                hpl[c] = hp_new
+            for t in blocks:
+                hp = psum.tile([P, ROWS], F32, name="hp", tag="bank")
                 for g in range(2):
                     nc.tensor.matmul_mx(
                         out=hp[:],
@@ -156,19 +171,21 @@ def tile_embed_update_pa_t_kernel(tc, net_in, embeds, m, W1, b1, Wf, b_f, gamma,
                         start=(g == 0),
                         stop=(g == 1),
                     )
-                if (t, c % 2) in V_HP:
-                    nc.vector.tensor_scalar(out=hp_sb[:, t, :], in0=hp[:], scalar1=b1f[:, t:t + 1], scalar2=0.0,
-                                            op0=ALU.add, op1=ALU.max)
-                else:
-                    nc.scalar.activation(out=hp_sb[:, t, :], in_=hp[:], func=ACT.Relu, bias=b1f[:, t:t + 1], scale=1.0)
+                nc.scalar.activation(out=hpl[c][:, t, :], in_=hp[:], func=ACT.Relu, bias=b1f[:, t:t + 1], scale=1.0)
 
         def stage_d(c):
             hg = work.tile([P, ROWS, 4], BF16, name="hgr", align_bytes=64)
             hgr[c] = hg
+            v_rows = ROWS - P if c >= S_REGROUP_FROM else ROWS
             nc.vector.tensor_copy(
-                out=hg[:].rearrange("p (c i) t -> p c t i", i=4),
-                in_=hpl[c][:].rearrange("p t (c i) -> p c t i", i=4),
+                out=hg[:, 0:v_rows, :].rearrange("p (c i) t -> p c t i", i=4),
+                in_=hpl[c][:, :, 0:v_rows].rearrange("p t (c i) -> p c t i", i=4),
             )
+            if v_rows < ROWS:
+                nc.scalar.copy(
+                    out=hg[:, v_rows:ROWS, :].rearrange("p (c i) t -> p c t i", i=4),
+                    in_=hpl[c][:, :, v_rows:ROWS].rearrange("p t (c i) -> p c t i", i=4),
+                )
 
         def stage_e(c):
             hco = work.tile([P, ROWS], U32, name="hcod", align_bytes=64)
@@ -177,7 +194,7 @@ def tile_embed_update_pa_t_kernel(tc, net_in, embeds, m, W1, b1, Wf, b_f, gamma,
             nc.vector.quantize_mx(out=hco[:].bitcast(FP8X4), scales=hsc[:], in_=hgr[c][:].rearrange("p r t -> p (r t)"))
 
         def stage_f(c):
-            op = pso.tile([P, LPC, CH], F32, name="op")
+            op = psum.tile([P, LPC, CH], F32, name="op", tag="bank")
             opb[c] = op
             for l in range(LPC):
                 nc.tensor.matmul_mx(
@@ -192,14 +209,17 @@ def tile_embed_update_pa_t_kernel(tc, net_in, embeds, m, W1, b1, Wf, b_f, gamma,
             cols = slice(c * LPC, (c + 1) * LPC)
             nc.scalar.activation(out=sig[:, cols], in_=op[:, :, OUT], func=ACT.Sigmoid, bias=bf127[:, 0:1], scale=1.0)
 
-        def stage_g(c):
+        def stage_gq(c):
+            b, kq = divmod(c, K // LPC)
+            cols = slice(c * LPC, (c + 1) * LPC)
+            ks = slice(kq * LPC, (kq + 1) * LPC)
+            nc.vector.tensor_tensor(out=gall[:, cols], in0=sig[:, cols], in1=mf[:, cols], op=ALU.mult)
+            nc.vector.scalar_tensor_tensor(out=sums_in[:, b, 2, ks], in0=gall[:, cols], scalar=LINK_EPS,
+                                           in1=mf[:, cols], op0=ALU.add, op1=ALU.mult)
+
+        def stage_stt(c):
             b, kq = divmod(c, K // LPC)
             op = opb[c]
-            cols = slice(c * LPC, (c + 1) * LPC)
-            q = sums_in[:, b, 2, kq * LPC:(kq + 1) * LPC]
-            nc.vector.tensor_tensor(out=gall[:, cols], in0=sig[:, cols], in1=mf[:, cols], op=ALU.mult)
-            nc.vector.scalar_tensor_tensor(out=q, in0=gall[:, cols], scalar=LINK_EPS, in1=mf[:, cols],
-                                           op0=ALU.add, op1=ALU.mult)
             if kq == 0:
                 acc_b = small.tile([P, 2, CH], F32, name="acc")
                 acc[b] = acc_b
@@ -212,7 +232,9 @@ def tile_embed_update_pa_t_kernel(tc, net_in, embeds, m, W1, b1, Wf, b_f, gamma,
                     nc.vector.scalar_tensor_tensor(out=a[:, l % 2, :], in0=op[:, l, :], scalar=qs, in1=a[:, l % 2, :],
                                                    op0=ALU.mult, op1=ALU.add)
 
-        def stage_ln(b):
+        ln_y1, ln_rstd = {}, {}
+
+        def stage_ln1(b):
             g16 = gall[:, b * K:(b + 1) * K]
             nc.vector.tensor_scalar_add(out=sums_in[:, b, 0, :], in0=g16, scalar1=LINK_EPS)
             nc.vector.tensor_tensor(out=sums_in[:, b, 1, :], in0=sums_in[:, b, 0, :], in1=g16, op=ALU.mult)
@@ -244,30 +266,51 @@ def tile_embed_update_pa_t_kernel(tc, net_in, embeds, m, W1, b1, Wf, b_f, gamma,
             y1 = small.tile([P, OUT], F32, name="y1")
             nc.vector.scalar_tensor_tensor(out=y1[:], in0=e2[:], scalar=mv[:, 0:1], in1=gmb[:, 0:OUT],
                                            op0=ALU.subtract, op1=ALU.mult)
+            ln_y1[b], ln_rstd[b] = y1, rstd
+
+        def stage_ln2(b):
             y2 = small.tile([P, OUT], F32, name="y2")
-            nc.vector.scalar_tensor_tensor(out=y2[:], in0=y1[:], scalar=rstd[:, 0:1], in1=btb[:, 0:OUT],
+            nc.vector.scalar_tensor_tensor(out=y2[:], in0=ln_y1[b][:], scalar=ln_rstd[b][:, 0:1], in1=btb[:, 0:OUT],
                                            op0=ALU.mult, op1=ALU.add)
             nc.sync.dma_start(out=out[b], in_=y2[:])
 
         def on(c):
             return 0 <= c < NCH
 
-        stage_a(0)
-        stage_b(0)
-        for i in range(NCH + 3):
-            if on(i + 1):
-                stage_a(i + 1)
-            if on(i):
-                stage_c(i)
-            if on(i - 1):
-                stage_d(i - 1)
-            if on(i - 2):
-                stage_g(i - 2)
-                if (i - 2) % (K // LPC) == K // LPC - 1:
-                    stage_ln((i - 2) // (K // LPC))
-            if on(i - 1):
-                stage_e(i - 1)
-            if on(i + 1):
-                stage_b(i + 1)
-            if on(i - 1):
-                stage_f(i - 1)
+        cpb = K // LPC
+
+        def chunk_closed(k):
+            if on(k - M2_LAG):
+                stage_f(k - M2_LAG)
+            if on(k - 1):
+                stage_d(k - 1)
+            j = k - M2_LAG - 1
+            if on(j):
+                stage_gq(j)
+                stage_stt(j)
+            if on(j - 1) and j % cpb == 0:
+                stage_ln2((j - 1) // cpb)
+            if on(j) and j % cpb == cpb - 1:
+                stage_ln1(j // cpb)
+            if on(k - 1):
+                stage_e(k - 1)
+
+        def h_bank(n):
+            k, t = divmod(n, 4)
+            stage_c(k, (t,))
+            if t == 3:
+                chunk_closed(k)
+
+        for c in range(NCH):
+            stage_a(c, (0, 1, 2, 3))
+            if c == 0:
+                prepare_weights()
+            if c >= 1:
+                stage_b(c - 1)
+            if c >= UNIT_LAG:
+                h_bank(c - UNIT_LAG)
+        stage_b(NCH - 1)
+        for n in range(NCH - UNIT_LAG, 4 * NCH):
+            h_bank(n)
+        for k in range(NCH, NCH + M2_LAG + 2):
+            chunk_closed(k)

@@ -25,7 +25,8 @@ FLOPS = 2 * B * S * K * IN * HID + 2 * B * S * K * HID * CH
 
 UNIT_LAG = 2
 M2_LAG = 2
-S_REGROUP_FROM = 3
+PIECES = tuple((c, 0, LPC) for c in range(NCH - 1)) + ((NCH - 1, 0, 2), (NCH - 1, 2, 1), (NCH - 1, 3, 1))
+NP = len(PIECES)
 
 
 def tile_embed_update_pa_t_kernel(tc, net_in, embeds, m, W1, b1, Wf, b_f, gamma, beta, out):
@@ -78,10 +79,16 @@ def tile_embed_update_pa_t_kernel(tc, net_in, embeds, m, W1, b1, Wf, b_f, gamma,
         nc.vector.memset(neghalf[:], -0.5)
         ones = const.tile([P, P], BF16)
         nc.vector.memset(ones[:], 1.0)
-        spread_ps = psum.tile([P, 4, CH], F32, name="spread_ps", tag="bank")
-        nc.tensor.matmul(out=spread_ps[:], lhsT=ones[:], rhs=rows3[:], start=True, stop=True)
         spread = const.tile([P, 3, CH], F32)
-        nc.vector.tensor_copy(out=spread[:], in_=spread_ps[:, 0:3, :])
+        eps_ln = const.tile([P, 1], F32)
+        nc.vector.memset(eps_ln[:], LN_EPS)
+
+        def spread_rows():
+            spread_ps = psum.tile([P, 4, CH], F32, name="spread_ps", tag="bank")
+            nc.tensor.matmul(out=spread_ps[:], lhsT=ones[:], rhs=rows3[:], start=True, stop=True)
+            nc.vector.tensor_copy(out=spread[:], in_=spread_ps[:, 0:3, :])
+            nc.vector.tensor_copy(out=bf127[:], in_=bfb[:, OUT:CH])
+
         bfb = spread[:, 0, :]
         gmb = spread[:, 1, :]
         btb = spread[:, 2, :]
@@ -114,11 +121,11 @@ def tile_embed_update_pa_t_kernel(tc, net_in, embeds, m, W1, b1, Wf, b_f, gamma,
             nc.vector.tensor_copy(out=b1f[:], in_=b1raw[:])
             quantise_w1(0)
             nc.vector.tensor_copy(out=wfg[:], in_=wfraw[:].rearrange("p t c -> p c t"))
-            nc.vector.tensor_copy(out=bf127[:], in_=bfb[:, OUT:CH])
             nc.vector.tensor_copy(out=mf[:], in_=msb[:].rearrange("p b k -> p (b k)"))
             nc.vector.quantize_mx(out=wfc[:].bitcast(FP8X4), scales=wfs[:], in_=wfg[:].rearrange("p c t -> p (c t)"))
             quantise_w1(1)
 
+        junk = const.tile([P, 1], F32)
         sig = const.tile([P, B * K], F32)
         gall = const.tile([P, B * K], F32)
         sums_in = const.tile([P, B, 3, K], F32)
@@ -155,81 +162,99 @@ def tile_embed_update_pa_t_kernel(tc, net_in, embeds, m, W1, b1, Wf, b_f, gamma,
                 in_=gnet[c][:].rearrange("p g r u -> p (g r u)").bitcast(BF16),
             )
 
-        def stage_c(c, blocks):
-            if c not in hpl:
+        def stage_c(n, t):
+            c, l0, nl = PIECES[n]
+            if n not in hpl:
                 hp_new = work.tile([P, 4, ROWS], BF16, name="hpl")
-                hpl[c] = hp_new
-            for t in blocks:
-                hp = psum.tile([P, ROWS], F32, name="hp", tag="bank")
-                for g in range(2):
-                    nc.tensor.matmul_mx(
-                        out=hp[:],
-                        lhsT=w1c[:, g, t * P:(t + 1) * P].bitcast(FP8X4),
-                        lhsT_scale=w1s[:, g, t * P:(t + 1) * P],
-                        rhs=ncod[c][:, g, :].bitcast(FP8X4),
-                        rhs_scale=nsca[c][:, g, :],
-                        start=(g == 0),
-                        stop=(g == 1),
-                    )
-                nc.scalar.activation(out=hpl[c][:, t, :], in_=hp[:], func=ACT.Relu, bias=b1f[:, t:t + 1], scale=1.0)
-
-        def stage_d(c):
-            hg = work.tile([P, ROWS, 4], BF16, name="hgr", align_bytes=64)
-            hgr[c] = hg
-            v_rows = ROWS - P if c >= S_REGROUP_FROM else ROWS
-            nc.vector.tensor_copy(
-                out=hg[:, 0:v_rows, :].rearrange("p (c i) t -> p c t i", i=4),
-                in_=hpl[c][:, :, 0:v_rows].rearrange("p t (c i) -> p c t i", i=4),
-            )
-            if v_rows < ROWS:
-                nc.scalar.copy(
-                    out=hg[:, v_rows:ROWS, :].rearrange("p (c i) t -> p c t i", i=4),
-                    in_=hpl[c][:, :, v_rows:ROWS].rearrange("p t (c i) -> p c t i", i=4),
+                hpl[n] = hp_new
+            rows = slice(l0 * P, (l0 + nl) * P)
+            hp = psum.tile([P, ROWS], F32, name="hp", tag="bank")
+            for g in range(2):
+                nc.tensor.matmul_mx(
+                    out=hp[:, 0:nl * P],
+                    lhsT=w1c[:, g, t * P:(t + 1) * P].bitcast(FP8X4),
+                    lhsT_scale=w1s[:, g, t * P:(t + 1) * P],
+                    rhs=ncod[c][:, g, rows].bitcast(FP8X4),
+                    rhs_scale=nsca[c][:, g, rows],
+                    start=(g == 0),
+                    stop=(g == 1),
                 )
+            nc.scalar.activation(out=hpl[n][:, t, 0:nl * P], in_=hp[:, 0:nl * P], func=ACT.Relu,
+                                 bias=b1f[:, t:t + 1], scale=1.0)
 
-        def stage_e(c):
+        def regroup(n, r0, r1, on_gpsimd):
+            dst = hgr[n][:, r0:r1, :].rearrange("p (c i) t -> p c t i", i=4)
+            src = hpl[n][:, :, r0:r1].rearrange("p t (c i) -> p c t i", i=4)
+            if on_gpsimd:
+                nc.gpsimd.tensor_scalar(out=dst, in0=src, scalar1=1.0, scalar2=0.0, op0=ALU.mult, op1=ALU.add)
+            else:
+                nc.vector.tensor_copy(out=dst, in_=src)
+
+        def stage_d(n):
+            nl = PIECES[n][2]
+            hg = work.tile([P, ROWS, 4], BF16, name="hgr", align_bytes=64)
+            hgr[n] = hg
+            if nl == LPC:
+                regroup(n, ROWS - P, ROWS, True)
+                regroup(n, 0, ROWS - P, False)
+            else:
+                regroup(n, 0, nl * P, False)
+
+        def stage_e(n):
+            nl = PIECES[n][2]
             hco = work.tile([P, ROWS], U32, name="hcod", align_bytes=64)
             hsc = work.tile([P, ROWS], U8, name="hsca", align_bytes=64)
-            hcod[c], hsca[c] = hco, hsc
-            nc.vector.quantize_mx(out=hco[:].bitcast(FP8X4), scales=hsc[:], in_=hgr[c][:].rearrange("p r t -> p (r t)"))
+            hcod[n], hsca[n] = hco, hsc
+            nc.vector.quantize_mx(out=hco[:, 0:nl * P].bitcast(FP8X4), scales=hsc[:, 0:nl * P],
+                                  in_=hgr[n][:, 0:nl * P, :].rearrange("p r t -> p (r t)"))
 
-        def stage_f(c):
+        def links(n):
+            c, l0, nl = PIECES[n]
+            return c * LPC + l0, nl
+
+        def stage_f(n):
+            first, nl = links(n)
             op = psum.tile([P, LPC, CH], F32, name="op", tag="bank")
-            opb[c] = op
-            for l in range(LPC):
+            opb[n] = op
+            for l in range(nl):
                 nc.tensor.matmul_mx(
                     out=op[:, l, :],
-                    lhsT=hcod[c][:, l * P:(l + 1) * P].bitcast(FP8X4),
-                    lhsT_scale=hsca[c][:, l * P:(l + 1) * P],
+                    lhsT=hcod[n][:, l * P:(l + 1) * P].bitcast(FP8X4),
+                    lhsT_scale=hsca[n][:, l * P:(l + 1) * P],
                     rhs=wfc[:].bitcast(FP8X4),
                     rhs_scale=wfs[:],
                     start=True,
                     stop=True,
                 )
-            cols = slice(c * LPC, (c + 1) * LPC)
-            nc.scalar.activation(out=sig[:, cols], in_=op[:, :, OUT], func=ACT.Sigmoid, bias=bf127[:, 0:1], scale=1.0)
+            nc.scalar.activation(out=sig[:, first:first + nl], in_=op[:, 0:nl, OUT], func=ACT.Sigmoid,
+                                 bias=bf127[:, 0:1], scale=1.0)
+            if n == NP - 1:
+                nc.scalar.activation(out=junk[:], in_=sig[:, first:first + 1], func=ACT.Abs_reciprocal_sqrt,
+                                     bias=eps_ln[:, 0:1], scale=1.0)
 
-        def stage_gq(c):
-            b, kq = divmod(c, K // LPC)
-            cols = slice(c * LPC, (c + 1) * LPC)
-            ks = slice(kq * LPC, (kq + 1) * LPC)
+        def stage_gq(n):
+            first, nl = links(n)
+            b, k0 = divmod(first, K)
+            cols = slice(first, first + nl)
             nc.vector.tensor_tensor(out=gall[:, cols], in0=sig[:, cols], in1=mf[:, cols], op=ALU.mult)
-            nc.vector.scalar_tensor_tensor(out=sums_in[:, b, 2, ks], in0=gall[:, cols], scalar=LINK_EPS,
+            nc.vector.scalar_tensor_tensor(out=sums_in[:, b, 2, k0:k0 + nl], in0=gall[:, cols], scalar=LINK_EPS,
                                            in1=mf[:, cols], op0=ALU.add, op1=ALU.mult)
 
-        def stage_stt(c):
-            b, kq = divmod(c, K // LPC)
-            op = opb[c]
-            if kq == 0:
+        def stage_stt(n):
+            first, nl = links(n)
+            b, k0 = divmod(first, K)
+            op = opb[n]
+            if k0 == 0:
                 acc_b = small.tile([P, 2, CH], F32, name="acc")
                 acc[b] = acc_b
             a = acc[b]
-            for l in range(LPC):
-                qs = sums_in[:, b, 2, kq * LPC + l:kq * LPC + l + 1]
-                if kq == 0 and l < 2:
-                    nc.vector.tensor_scalar(out=a[:, l % 2, :], in0=op[:, l, :], scalar1=qs, scalar2=None, op0=ALU.mult)
+            for l in range(nl):
+                k = k0 + l
+                qs = sums_in[:, b, 2, k:k + 1]
+                if k < 2:
+                    nc.vector.tensor_scalar(out=a[:, k % 2, :], in0=op[:, l, :], scalar1=qs, scalar2=None, op0=ALU.mult)
                 else:
-                    nc.vector.scalar_tensor_tensor(out=a[:, l % 2, :], in0=op[:, l, :], scalar=qs, in1=a[:, l % 2, :],
+                    nc.vector.scalar_tensor_tensor(out=a[:, k % 2, :], in0=op[:, l, :], scalar=qs, in1=a[:, k % 2, :],
                                                    op0=ALU.mult, op1=ALU.add)
 
         ln_y1, ln_rstd = {}, {}
@@ -237,32 +262,35 @@ def tile_embed_update_pa_t_kernel(tc, net_in, embeds, m, W1, b1, Wf, b_f, gamma,
         def stage_ln1(b):
             g16 = gall[:, b * K:(b + 1) * K]
             nc.vector.tensor_scalar_add(out=sums_in[:, b, 0, :], in0=g16, scalar1=LINK_EPS)
-            nc.vector.tensor_tensor(out=sums_in[:, b, 1, :], in0=sums_in[:, b, 0, :], in1=g16, op=ALU.mult)
+            nc.vector.scalar_tensor_tensor(out=sums_in[:, b, 1, :], in0=g16, scalar=LINK_EPS, in1=g16,
+                                           op0=ALU.add, op1=ALU.mult)
             sums = small.tile([P, 3], F32, name="sums")
             nc.vector.tensor_reduce(out=sums[:], in_=sums_in[:, b], axis=AX.X, op=ALU.add)
             rl = small.tile([P, 1], F32, name="rl")
             nc.vector.reciprocal(out=rl[:], in_=sums[:, 0:1])
-            s12 = small.tile([P, 2], F32, name="s12")
-            nc.vector.tensor_scalar(out=s12[:, 0:1], in0=sums[:, 1:2], scalar1=rl[:, 0:1], scalar2=rl[:, 0:1],
+            w0 = small.tile([P, OUT], F32, name="w0")
+            nc.vector.scalar_tensor_tensor(out=w0[:], in0=bfb[:, 0:OUT], scalar=sums[:, 2:3], in1=acc[b][:, 0, 0:OUT],
+                                           op0=ALU.mult, op1=ALU.add)
+            s1 = small.tile([P, 1], F32, name="s1")
+            nc.vector.tensor_scalar(out=s1[:], in0=sums[:, 1:2], scalar1=rl[:, 0:1], scalar2=rl[:, 0:1],
                                     op0=ALU.mult, op1=ALU.mult)
-            nc.vector.tensor_tensor(out=s12[:, 1:2], in0=s12[:, 0:1], in1=sums[:, 2:3], op=ALU.mult)
-            e0 = small.tile([P, OUT], F32, name="e0")
-            nc.vector.scalar_tensor_tensor(out=e0[:], in0=bfb[:, 0:OUT], scalar=s12[:, 1:2], in1=emb[:, b, 0:OUT],
-                                           op0=ALU.mult, op1=ALU.add)
-            e1 = small.tile([P, OUT], F32, name="e1")
-            nc.vector.scalar_tensor_tensor(out=e1[:], in0=acc[b][:, 0, 0:OUT], scalar=s12[:, 0:1], in1=e0[:],
-                                           op0=ALU.mult, op1=ALU.add)
+            w1 = small.tile([P, OUT], F32, name="w1")
+            nc.vector.tensor_tensor(out=w1[:], in0=w0[:], in1=acc[b][:, 1, 0:OUT], op=ALU.add)
             e2 = small.tile([P, OUT], F32, name="e2")
-            nc.vector.scalar_tensor_tensor(out=e2[:], in0=acc[b][:, 1, 0:OUT], scalar=s12[:, 0:1], in1=e1[:],
+            nc.vector.scalar_tensor_tensor(out=e2[:], in0=w1[:], scalar=s1[:, 0:1], in1=emb[:, b, 0:OUT],
                                            op0=ALU.mult, op1=ALU.add)
             st6 = small.tile([P, 6], F32, name="st6")
             nc.vector.bn_stats(out=st6[:], in_=e2[:])
             mv = small.tile([P, 2], F32, name="mv")
             nc.vector.bn_aggr(out=mv[:], in_=st6[:])
-            vpe = small.tile([P, 1], F32, name="vpe")
-            nc.gpsimd.tensor_scalar_add(out=vpe[:], in0=mv[:, 1:2], scalar1=LN_EPS)
             rstd = small.tile([P, 1], F32, name="rstd")
-            nc.gpsimd.tensor_tensor(out=rstd[:], in0=vpe[:], in1=neghalf[:], op=ALU.pow)
+            if b == B - 1:
+                nc.scalar.activation(out=rstd[:], in_=mv[:, 1:2], func=ACT.Abs_reciprocal_sqrt,
+                                     bias=eps_ln[:, 0:1], scale=1.0)
+            else:
+                vpe = small.tile([P, 1], F32, name="vpe")
+                nc.gpsimd.tensor_scalar_add(out=vpe[:], in0=mv[:, 1:2], scalar1=LN_EPS)
+                nc.gpsimd.tensor_tensor(out=rstd[:], in0=vpe[:], in1=neghalf[:], op=ALU.pow)
             y1 = small.tile([P, OUT], F32, name="y1")
             nc.vector.scalar_tensor_tensor(out=y1[:], in0=e2[:], scalar=mv[:, 0:1], in1=gmb[:, 0:OUT],
                                            op0=ALU.subtract, op1=ALU.mult)
@@ -274,43 +302,47 @@ def tile_embed_update_pa_t_kernel(tc, net_in, embeds, m, W1, b1, Wf, b_f, gamma,
                                            op0=ALU.mult, op1=ALU.add)
             nc.sync.dma_start(out=out[b], in_=y2[:])
 
-        def on(c):
-            return 0 <= c < NCH
+        def on(n):
+            return 0 <= n < NP
 
-        cpb = K // LPC
+        def ends_batch(n):
+            first, nl = links(n)
+            return (first + nl) % K == 0
 
-        def chunk_closed(k):
-            if on(k - M2_LAG):
-                stage_f(k - M2_LAG)
-            if on(k - 1):
-                stage_d(k - 1)
-            j = k - M2_LAG - 1
+        def piece_closed(n):
+            if on(n - M2_LAG):
+                stage_f(n - M2_LAG)
+            if on(n - 1):
+                stage_d(n - 1)
+            j = n - M2_LAG - 1
             if on(j):
                 stage_gq(j)
                 stage_stt(j)
-            if on(j - 1) and j % cpb == 0:
-                stage_ln2((j - 1) // cpb)
-            if on(j) and j % cpb == cpb - 1:
-                stage_ln1(j // cpb)
-            if on(k - 1):
-                stage_e(k - 1)
+            if on(j - 1) and ends_batch(j - 1):
+                stage_ln2(links(j - 1)[0] // K)
+            if on(j) and ends_batch(j):
+                stage_ln1(links(j)[0] // K)
+            if on(n - 1):
+                stage_e(n - 1)
 
-        def h_bank(n):
-            k, t = divmod(n, 4)
-            stage_c(k, (t,))
+        def h_bank(i):
+            n, t = divmod(i, 4)
+            stage_c(n, t)
             if t == 3:
-                chunk_closed(k)
+                piece_closed(n)
 
         for c in range(NCH):
             stage_a(c, (0, 1, 2, 3))
             if c == 0:
                 prepare_weights()
+            if c == 1:
+                spread_rows()
             if c >= 1:
                 stage_b(c - 1)
             if c >= UNIT_LAG:
                 h_bank(c - UNIT_LAG)
         stage_b(NCH - 1)
-        for n in range(NCH - UNIT_LAG, 4 * NCH):
-            h_bank(n)
-        for k in range(NCH, NCH + M2_LAG + 2):
-            chunk_closed(k)
+        for i in range(NCH - UNIT_LAG, 4 * NP):
+            h_bank(i)
+        for n in range(NP, NP + M2_LAG + 2):
+            piece_closed(n)

@@ -25,6 +25,7 @@ FLOPS = 2 * B * S * K * IN * HID + 2 * B * S * K * HID * CH
 
 UNIT_LAG = 2
 M2_LAG = 2
+S_REGROUP_FROM = 3
 PIECES = tuple((c, 0, LPC) for c in range(NCH - 1)) + ((NCH - 1, 0, 2), (NCH - 1, 2, 1), (NCH - 1, 3, 1))
 NP = len(PIECES)
 
@@ -40,15 +41,22 @@ def tile_embed_update_pa_t_kernel(tc, net_in, embeds, m, W1, b1, Wf, b_f, gamma,
         small = ctx.enter_context(tc.tile_pool(name="small", bufs=2))
         psum = ctx.enter_context(tc.psum_pool(name="psum", bufs=8))
 
+        junk = const.tile([P, 1], F32)
+        nc.vector.memset(junk[:], 0.0)
+        nc.scalar.activation(out=junk[:], in_=junk[:], func=ACT.Sigmoid)
+
         xin = {}
 
         def load(c):
             b, kq = divmod(c, K // LPC)
             xt_in = xpool.tile([P, LPC * IN], BF16, name="xin")
-            nc.sync.dma_start(
-                out=xt_in[:],
-                in_=net_in[b].rearrange("s k i -> s (k i)")[:, kq * LPC * IN:(kq + 1) * LPC * IN],
-            )
+            cuts = 2 if c == 0 else 1
+            width = LPC * IN // cuts
+            for h in range(cuts):
+                nc.sync.dma_start(
+                    out=xt_in[:, h * width:(h + 1) * width],
+                    in_=net_in[b].rearrange("s k i -> s (k i)")[:, kq * LPC * IN + h * width:kq * LPC * IN + (h + 1) * width],
+                )
             xin[c] = xt_in
 
         load(0)
@@ -125,7 +133,6 @@ def tile_embed_update_pa_t_kernel(tc, net_in, embeds, m, W1, b1, Wf, b_f, gamma,
             nc.vector.quantize_mx(out=wfc[:].bitcast(FP8X4), scales=wfs[:], in_=wfg[:].rearrange("p c t -> p (c t)"))
             quantise_w1(1)
 
-        junk = const.tile([P, 1], F32)
         sig = const.tile([P, B * K], F32)
         gall = const.tile([P, B * K], F32)
         sums_in = const.tile([P, B, 3, K], F32)
@@ -139,7 +146,7 @@ def tile_embed_update_pa_t_kernel(tc, net_in, embeds, m, W1, b1, Wf, b_f, gamma,
                 gnet[c] = gn_new
             gn = gnet[c]
             for j in banks:
-                g, lp = divmod(j, 2)
+                lp, g = divmod(j, 2)
                 xt = psum.tile([P, 2, 2 * P], F32, name="xt", tag="bank")
                 for u in range(2):
                     for li in range(2):
@@ -182,23 +189,21 @@ def tile_embed_update_pa_t_kernel(tc, net_in, embeds, m, W1, b1, Wf, b_f, gamma,
             nc.scalar.activation(out=hpl[n][:, t, 0:nl * P], in_=hp[:, 0:nl * P], func=ACT.Relu,
                                  bias=b1f[:, t:t + 1], scale=1.0)
 
-        def regroup(n, r0, r1, on_gpsimd):
-            dst = hgr[n][:, r0:r1, :].rearrange("p (c i) t -> p c t i", i=4)
-            src = hpl[n][:, :, r0:r1].rearrange("p t (c i) -> p c t i", i=4)
-            if on_gpsimd:
-                nc.gpsimd.tensor_scalar(out=dst, in0=src, scalar1=1.0, scalar2=0.0, op0=ALU.mult, op1=ALU.add)
-            else:
-                nc.vector.tensor_copy(out=dst, in_=src)
+        def regroup(copy, n, r0, r1):
+            copy(
+                out=hgr[n][:, r0:r1, :].rearrange("p (c i) t -> p c t i", i=4),
+                in_=hpl[n][:, :, r0:r1].rearrange("p t (c i) -> p c t i", i=4),
+            )
 
         def stage_d(n):
             nl = PIECES[n][2]
             hg = work.tile([P, ROWS, 4], BF16, name="hgr", align_bytes=64)
             hgr[n] = hg
-            if nl == LPC:
-                regroup(n, ROWS - P, ROWS, True)
-                regroup(n, 0, ROWS - P, False)
+            if nl == LPC and n >= S_REGROUP_FROM:
+                regroup(nc.vector.tensor_copy, n, 0, ROWS - P)
+                regroup(nc.scalar.copy, n, ROWS - P, ROWS)
             else:
-                regroup(n, 0, nl * P, False)
+                regroup(nc.vector.tensor_copy, n, 0, nl * P)
 
         def stage_e(n):
             nl = PIECES[n][2]

@@ -336,17 +336,18 @@ def tile_embed_update_pa_t_kernel(tc, net_in, embeds, m, W1, b1, Wf, b_f, gamma,
             if t == 3:
                 piece_closed(n)
 
-        for c in range(NCH):
-            stage_a(c, (0, 1, 2, 3))
-            if c == 0:
-                prepare_weights()
-            if c == 1:
-                spread_rows()
-            if c >= 1:
-                stage_b(c - 1)
-            if c >= UNIT_LAG:
-                h_bank(c - UNIT_LAG)
-        stage_b(NCH - 1)
+        with tc.manual_schedule():
+            for c in range(NCH):
+                stage_a(c, (0, 1, 2, 3))
+                if c == 0:
+                    prepare_weights()
+                if c == 1:
+                    spread_rows()
+                if c >= 1:
+                    stage_b(c - 1)
+                if c >= UNIT_LAG:
+                    h_bank(c - UNIT_LAG)
+            stage_b(NCH - 1)
         for i in range(NCH - UNIT_LAG, 4 * NP):
             h_bank(i)
         for n in range(NP, NP + M2_LAG + 2):

from contextlib import ExitStack

import concourse.mybir as mybir
from concourse.masks import make_identity

F32 = mybir.dt.float32
BF16 = mybir.dt.bfloat16
U32 = mybir.dt.uint32
U8 = mybir.dt.uint8
FP8X4 = mybir.dt.float8_e4m3fn_x4
ALU = mybir.AluOpType
ACT = mybir.ActivationFunctionType
AX = mybir.AxisListType

P = 128
B, S, K, IN, HID, OUT = 4, 128, 16, 1024, 512, 127
CH = OUT + 1
LPC = 4
NCH = B * K // LPC
ROWS = LPC * P
LN_EPS = 1e-5
LINK_EPS = 1e-8

FLOPS = 2 * B * S * K * IN * HID + 2 * B * S * K * HID * CH

UNIT_LAG = 2
M2_LAG = 2
S_REGROUP_FROM = 3
PIECES = tuple((c, 0, LPC) for c in range(NCH - 1)) + ((NCH - 1, 0, 2), (NCH - 1, 2, 1), (NCH - 1, 3, 1))
NP = len(PIECES)


def tile_embed_update_pa_t_kernel(tc, net_in, embeds, m, W1, b1, Wf, b_f, gamma, beta, out):
    nc = tc.nc
    with ExitStack() as ctx:
        const = ctx.enter_context(tc.tile_pool(name="const", bufs=1))
        xpool = ctx.enter_context(tc.tile_pool(name="xpool", bufs=5))
        gpool = ctx.enter_context(tc.tile_pool(name="gpool", bufs=3))
        net = ctx.enter_context(tc.tile_pool(name="net", bufs=14))
        work = ctx.enter_context(tc.tile_pool(name="work", bufs=3))
        small = ctx.enter_context(tc.tile_pool(name="small", bufs=2))
        psum = ctx.enter_context(tc.psum_pool(name="psum", bufs=8))

        junk = const.tile([P, 1], F32)
        nc.vector.memset(junk[:], 0.0)
        nc.scalar.activation(out=junk[:], in_=junk[:], func=ACT.Sigmoid)

        xin = {}

        def load(c):
            b, kq = divmod(c, K // LPC)
            xt_in = xpool.tile([P, LPC * IN], BF16, name="xin")
            cuts = 2 if c == 0 else 1
            width = LPC * IN // cuts
            for h in range(cuts):
                nc.sync.dma_start(
                    out=xt_in[:, h * width:(h + 1) * width],
                    in_=net_in[b].rearrange("s k i -> s (k i)")[:, kq * LPC * IN + h * width:kq * LPC * IN + (h + 1) * width],
                )
            xin[c] = xt_in

        load(0)
        w1raw = const.tile([P, 8, HID], BF16)
        nc.sync.dma_start(
            out=w1raw[:].rearrange("p (a e) h -> p a (e h)", e=2),
            in_=W1.rearrange("(a p e) h -> p a (e h)", a=4, p=P, e=2),
        )
        b1raw = const.tile([P, 4], BF16)
        nc.scalar.dma_start(out=b1raw[:], in_=b1.rearrange("(q t) -> q t", t=4))
        wfraw = const.tile([P, 4, CH], BF16)
        nc.scalar.dma_start(out=wfraw[:].rearrange("p t c -> p (t c)"), in_=Wf.rearrange("(q t) c -> q (t c)", t=4))
        rows3 = const.tile([P, 4, CH], BF16)
        nc.vector.memset(rows3[:], 0.0)
        nc.scalar.dma_start(out=rows3[0:1, 0, :], in_=b_f.unsqueeze(0))
        nc.scalar.dma_start(out=rows3[0:1, 1, 0:OUT], in_=gamma.unsqueeze(0))
        nc.scalar.dma_start(out=rows3[0:1, 2, 0:OUT], in_=beta.unsqueeze(0))
        msb = const.tile([P, B, K], BF16)
        nc.scalar.dma_start(out=msb[:], in_=m.rearrange("b s k o -> s b (k o)"))
        emb = const.tile([P, B, CH], BF16)
        nc.scalar.dma_start(out=emb[:, :, 0:OUT], in_=embeds.rearrange("b s c -> s b c"))
        for c in range(1, NCH):
            load(c)

        ident = const.tile([P, P], F32)
        make_identity(nc, ident[:])
        neghalf = const.tile([P, 1], F32)
        nc.vector.memset(neghalf[:], -0.5)
        ones = const.tile([P, P], BF16)
        nc.vector.memset(ones[:], 1.0)
        spread = const.tile([P, 3, CH], F32)
        eps_ln = const.tile([P, 1], F32)
        nc.vector.memset(eps_ln[:], LN_EPS)

        def spread_rows():
            spread_ps = psum.tile([P, 4, CH], F32, name="spread_ps", tag="bank")
            nc.tensor.matmul(out=spread_ps[:], lhsT=ones[:], rhs=rows3[:], start=True, stop=True)
            nc.vector.tensor_copy(out=spread[:], in_=spread_ps[:, 0:3, :])
            nc.vector.tensor_copy(out=bf127[:], in_=bfb[:, OUT:CH])

        bfb = spread[:, 0, :]
        gmb = spread[:, 1, :]
        btb = spread[:, 2, :]

        w1g = const.tile([P, 2, HID, 4], BF16, align_bytes=64)
        w1c = const.tile([P, 2, HID], U32, align_bytes=64)
        w1s = const.tile([P, 2, HID], U8, align_bytes=64)
        b1f = const.tile([P, 4], F32)
        wfg = const.tile([P, CH, 4], BF16, align_bytes=64)
        bf127 = const.tile([P, 1], F32)
        mf = const.tile([P, B * K], F32)
        wfc = const.tile([P, CH], U32, align_bytes=64)
        wfs = const.tile([P, CH], U8, align_bytes=64)

        def quantise_w1(g):
            nc.vector.quantize_mx(
                out=w1c[:, g, :].bitcast(FP8X4),
                scales=w1s[:, g, :],
                in_=w1g[:, g].rearrange("p h j -> p (h j)"),
            )

        def prepare_weights():
            for g in range(2):
                src = w1raw[:, 4 * g:4 * g + 4, :].rearrange("p j (q t) -> p t q j", t=4)
                dst = w1g[:, g].rearrange("p (t q) j -> p t q j", t=4)
                if g == 0:
                    nc.vector.tensor_copy(out=dst, in_=src)
                else:
                    nc.scalar.copy(out=dst, in_=src)
            nc.vector.tensor_copy(out=b1f[:], in_=b1raw[:])
            quantise_w1(0)
            nc.vector.tensor_copy(out=wfg[:], in_=wfraw[:].rearrange("p t c -> p c t"))
            nc.vector.tensor_copy(out=mf[:], in_=msb[:].rearrange("p b k -> p (b k)"))
            nc.vector.quantize_mx(out=wfc[:].bitcast(FP8X4), scales=wfs[:], in_=wfg[:].rearrange("p c t -> p (c t)"))
            quantise_w1(1)

        sig = const.tile([P, B * K], F32)
        gall = const.tile([P, B * K], F32)
        sums_in = const.tile([P, B, 3, K], F32)

        gnet, ncod, nsca, hpl, hgr, hcod, hsca, opb, acc = {}, {}, {}, {}, {}, {}, {}, {}, {}

        def stage_a(c, banks):
            xf = xin[c][:].bitcast(F32)
            if c not in gnet:
                gn_new = gpool.tile([P, 2, ROWS, 2], F32, name="gnet", align_bytes=64)
                gnet[c] = gn_new
            gn = gnet[c]
            for j in banks:
                lp, g = divmod(j, 2)
                xt = psum.tile([P, 2, 2 * P], F32, name="xt", tag="bank")
                for u in range(2):
                    for li in range(2):
                        col = (2 * lp + li) * (IN // 2) + g * 256 + u * P
                        nc.tensor.transpose(xt[:, u, li * P:(li + 1) * P], xf[:, col:col + P], ident[:])
                dst = gn[:, g, lp * 2 * P:(lp + 1) * 2 * P, :]
                src = xt[:].rearrange("p u r -> p r u")
                if j == 3:
                    nc.vector.tensor_copy(out=dst, in_=src)
                else:
                    nc.scalar.copy(out=dst, in_=src)

        def stage_b(c):
            nco = net.tile([P, 2, ROWS], U32, name="ncod", align_bytes=64)
            nsc = net.tile([P, 2, ROWS], U8, name="nsca", align_bytes=64)
            ncod[c], nsca[c] = nco, nsc
            nc.vector.quantize_mx(
                out=nco[:].rearrange("p g r -> p (g r)").bitcast(FP8X4),
                scales=nsc[:].rearrange("p g r -> p (g r)"),
                in_=gnet[c][:].rearrange("p g r u -> p (g r u)").bitcast(BF16),
            )

        def stage_c(n, t):
            c, l0, nl = PIECES[n]
            if n not in hpl:
                hp_new = work.tile([P, 4, ROWS], BF16, name="hpl")
                hpl[n] = hp_new
            rows = slice(l0 * P, (l0 + nl) * P)
            hp = psum.tile([P, ROWS], F32, name="hp", tag="bank")
            for g in range(2):
                nc.tensor.matmul_mx(
                    out=hp[:, 0:nl * P],
                    lhsT=w1c[:, g, t * P:(t + 1) * P].bitcast(FP8X4),
                    lhsT_scale=w1s[:, g, t * P:(t + 1) * P],
                    rhs=ncod[c][:, g, rows].bitcast(FP8X4),
                    rhs_scale=nsca[c][:, g, rows],
                    start=(g == 0),
                    stop=(g == 1),
                )
            nc.scalar.activation(out=hpl[n][:, t, 0:nl * P], in_=hp[:, 0:nl * P], func=ACT.Relu,
                                 bias=b1f[:, t:t + 1], scale=1.0)

        def regroup(copy, n, r0, r1):
            copy(
                out=hgr[n][:, r0:r1, :].rearrange("p (c i) t -> p c t i", i=4),
                in_=hpl[n][:, :, r0:r1].rearrange("p t (c i) -> p c t i", i=4),
            )

        def stage_d(n):
            nl = PIECES[n][2]
            hg = work.tile([P, ROWS, 4], BF16, name="hgr", align_bytes=64)
            hgr[n] = hg
            if nl == LPC and n >= S_REGROUP_FROM:
                regroup(nc.vector.tensor_copy, n, 0, ROWS - P)
                regroup(nc.scalar.copy, n, ROWS - P, ROWS)
            else:
                regroup(nc.vector.tensor_copy, n, 0, nl * P)

        def stage_e(n):
            nl = PIECES[n][2]
            hco = work.tile([P, ROWS], U32, name="hcod", align_bytes=64)
            hsc = work.tile([P, ROWS], U8, name="hsca", align_bytes=64)
            hcod[n], hsca[n] = hco, hsc
            nc.vector.quantize_mx(out=hco[:, 0:nl * P].bitcast(FP8X4), scales=hsc[:, 0:nl * P],
                                  in_=hgr[n][:, 0:nl * P, :].rearrange("p r t -> p (r t)"))

        def links(n):
            c, l0, nl = PIECES[n]
            return c * LPC + l0, nl

        def stage_f(n):
            first, nl = links(n)
            op = psum.tile([P, LPC, CH], F32, name="op", tag="bank")
            opb[n] = op
            for l in range(nl):
                nc.tensor.matmul_mx(
                    out=op[:, l, :],
                    lhsT=hcod[n][:, l * P:(l + 1) * P].bitcast(FP8X4),
                    lhsT_scale=hsca[n][:, l * P:(l + 1) * P],
                    rhs=wfc[:].bitcast(FP8X4),
                    rhs_scale=wfs[:],
                    start=True,
                    stop=True,
                )
            nc.scalar.activation(out=sig[:, first:first + nl], in_=op[:, 0:nl, OUT], func=ACT.Sigmoid,
                                 bias=bf127[:, 0:1], scale=1.0)
            if n == NP - 1:
                nc.scalar.activation(out=junk[:], in_=sig[:, first:first + 1], func=ACT.Abs_reciprocal_sqrt,
                                     bias=eps_ln[:, 0:1], scale=1.0)

        def stage_gq(n):
            first, nl = links(n)
            b, k0 = divmod(first, K)
            cols = slice(first, first + nl)
            nc.vector.tensor_tensor(out=gall[:, cols], in0=sig[:, cols], in1=mf[:, cols], op=ALU.mult)
            nc.vector.scalar_tensor_tensor(out=sums_in[:, b, 2, k0:k0 + nl], in0=gall[:, cols], scalar=LINK_EPS,
                                           in1=mf[:, cols], op0=ALU.add, op1=ALU.mult)

        def stage_stt(n):
            first, nl = links(n)
            b, k0 = divmod(first, K)
            op = opb[n]
            if k0 == 0:
                acc_b = small.tile([P, 2, CH], F32, name="acc")
                acc[b] = acc_b
            a = acc[b]
            for l in range(nl):
                k = k0 + l
                qs = sums_in[:, b, 2, k:k + 1]
                if k < 2:
                    nc.vector.tensor_scalar(out=a[:, k % 2, :], in0=op[:, l, :], scalar1=qs, scalar2=None, op0=ALU.mult)
                else:
                    nc.vector.scalar_tensor_tensor(out=a[:, k % 2, :], in0=op[:, l, :], scalar=qs, in1=a[:, k % 2, :],
                                                   op0=ALU.mult, op1=ALU.add)

        ln_y1, ln_rstd = {}, {}

        def stage_ln1(b):
            g16 = gall[:, b * K:(b + 1) * K]
            nc.vector.tensor_scalar_add(out=sums_in[:, b, 0, :], in0=g16, scalar1=LINK_EPS)
            nc.vector.scalar_tensor_tensor(out=sums_in[:, b, 1, :], in0=g16, scalar=LINK_EPS, in1=g16,
                                           op0=ALU.add, op1=ALU.mult)
            sums = small.tile([P, 3], F32, name="sums")
            nc.vector.tensor_reduce(out=sums[:], in_=sums_in[:, b], axis=AX.X, op=ALU.add)
            rl = small.tile([P, 1], F32, name="rl")
            nc.vector.reciprocal(out=rl[:], in_=sums[:, 0:1])
            w0 = small.tile([P, OUT], F32, name="w0")
            nc.vector.scalar_tensor_tensor(out=w0[:], in0=bfb[:, 0:OUT], scalar=sums[:, 2:3], in1=acc[b][:, 0, 0:OUT],
                                           op0=ALU.mult, op1=ALU.add)
            s1 = small.tile([P, 1], F32, name="s1")
            nc.vector.tensor_scalar(out=s1[:], in0=sums[:, 1:2], scalar1=rl[:, 0:1], scalar2=rl[:, 0:1],
                                    op0=ALU.mult, op1=ALU.mult)
            w1 = small.tile([P, OUT], F32, name="w1")
            nc.vector.tensor_tensor(out=w1[:], in0=w0[:], in1=acc[b][:, 1, 0:OUT], op=ALU.add)
            e2 = small.tile([P, OUT], F32, name="e2")
            nc.vector.scalar_tensor_tensor(out=e2[:], in0=w1[:], scalar=s1[:, 0:1], in1=emb[:, b, 0:OUT],
                                           op0=ALU.mult, op1=ALU.add)
            st6 = small.tile([P, 6], F32, name="st6")
            nc.vector.bn_stats(out=st6[:], in_=e2[:])
            mv = small.tile([P, 2], F32, name="mv")
            nc.vector.bn_aggr(out=mv[:], in_=st6[:])
            rstd = small.tile([P, 1], F32, name="rstd")
            if b == B - 1:
                nc.scalar.activation(out=rstd[:], in_=mv[:, 1:2], func=ACT.Abs_reciprocal_sqrt,
                                     bias=eps_ln[:, 0:1], scale=1.0)
            else:
                vpe = small.tile([P, 1], F32, name="vpe")
                nc.gpsimd.tensor_scalar_add(out=vpe[:], in0=mv[:, 1:2], scalar1=LN_EPS)
                nc.gpsimd.tensor_tensor(out=rstd[:], in0=vpe[:], in1=neghalf[:], op=ALU.pow)
            y1 = small.tile([P, OUT], F32, name="y1")
            nc.vector.scalar_tensor_tensor(out=y1[:], in0=e2[:], scalar=mv[:, 0:1], in1=gmb[:, 0:OUT],
                                           op0=ALU.subtract, op1=ALU.mult)
            ln_y1[b], ln_rstd[b] = y1, rstd

        def stage_ln2(b):
            y2 = small.tile([P, OUT], F32, name="y2")
            nc.vector.scalar_tensor_tensor(out=y2[:], in0=ln_y1[b][:], scalar=ln_rstd[b][:, 0:1], in1=btb[:, 0:OUT],
                                           op0=ALU.mult, op1=ALU.add)
            nc.sync.dma_start(out=out[b], in_=y2[:])

        def on(n):
            return 0 <= n < NP

        def ends_batch(n):
            first, nl = links(n)
            return (first + nl) % K == 0

        def piece_closed(n):
            if on(n - M2_LAG):
                stage_f(n - M2_LAG)
            if on(n - 1):
                stage_d(n - 1)
            j = n - M2_LAG - 1
            if on(j):
                stage_gq(j)
                stage_stt(j)
            if on(j - 1) and ends_batch(j - 1):
                stage_ln2(links(j - 1)[0] // K)
            if on(j) and ends_batch(j):
                stage_ln1(links(j)[0] // K)
            if on(n - 1):
                stage_e(n - 1)

        def h_bank(i):
            n, t = divmod(i, 4)
            stage_c(n, t)
            if t == 3:
                piece_closed(n)

        with tc.manual_schedule():
            for c in range(NCH):
                stage_a(c, (0, 1, 2, 3))
                if c == 0:
                    prepare_weights()
                if c == 1:
                    spread_rows()
                if c >= 1:
                    stage_b(c - 1)
                if c >= UNIT_LAG:
                    h_bank(c - UNIT_LAG)
            stage_b(NCH - 1)
        for i in range(NCH - UNIT_LAG, 4 * NP):
            h_bank(i)
        for n in range(NP, NP + M2_LAG + 2):
            piece_closed(n)
